import numpy as np
import ml_dtypes


def mxq(x, axis, fmt="e4m3"):
    dtype, down = {"e4m3": (ml_dtypes.float8_e4m3fn, 7), "e5m2": (ml_dtypes.float8_e5m2, 14)}[fmt]
    v = np.moveaxis(np.asarray(x, np.float32).astype(ml_dtypes.bfloat16).astype(np.float64), axis, -1)
    blocks = v.reshape(v.shape[:-1] + (-1, 32))
    amax = np.abs(blocks).max(-1, keepdims=True)
    byte = np.maximum(np.where(amax > 0, np.frexp(amax)[1] - 1 + 127, 0) - down, 1)
    scale = np.exp2(byte - 127.0)
    codes = (blocks / scale).astype(np.float32).astype(dtype).astype(np.float64)
    return np.moveaxis((codes * scale).reshape(v.shape), -1, axis)


WIDE = False


def mx_kscale(k):
    if not WIDE:
        return np.ones(k)
    levels = np.array([10, -10, 5, -5, 0])
    a = np.random.permutation(np.resize(levels, k // 512 * 4)).reshape(k // 512, 4)
    idx = np.arange(k)
    return np.exp2(a[idx // 512, idx % 128 // 32])


BF16 = ml_dtypes.bfloat16


def bf(x):
    return np.asarray(x, np.float32).astype(BF16)


def f64(x):
    return np.asarray(x).astype(np.float64)


H, L, B, S = 512, 2, 1024, 16


def sigmoid(v):
    return 1.0 / (1.0 + np.exp(-v))


def setup_inputs():
    r = np.random.standard_normal
    s, t, u = mx_kscale(H), mx_kscale(H), mx_kscale(H)
    st = np.concatenate([s, t])
    return {
        "x": bf(r((B, H)) * s),
        "enc_seq": bf(r((S, B, H)) * t),
        "attn_W": bf(r((H, H)) / np.sqrt(H) / s[None, :] / t[:, None]),
        "attn_b": bf(r(H) * 0.5 / t),
        "h_prev": bf(r((B, H)) * u),
        "c_prev": bf(r((B, H))),
        "W_ih0": bf(r((4 * H, H + H)) * 0.6 / np.sqrt(H) / st[None, :]),
        "W_hh0": bf(r((4 * H, H)) * 0.6 / np.sqrt(H) / u[None, :]),
        "b_ih0": bf(r(4 * H) * 0.3),
        "b_hh0": bf(r(4 * H) * 0.3),
    }


def reference(x, enc_seq, attn_W, attn_b, h_prev, c_prev, W_ih0, W_hh0, b_ih0, b_hh0):
    enc = f64(enc_seq)
    xq = mxq(f64(x), 1, "e4m3")
    attn_lin = (xq @ mxq(f64(attn_W).T, 0, "e4m3")) + f64(attn_b)
    scores = attn_lin[None, :, :] * enc
    e = np.exp(scores - scores.max(0, keepdims=True))
    w = e / e.sum(0, keepdims=True)
    attention = (enc * w).sum(0)
    aq = mxq(attention, 1, "e4m3")
    w_x = mxq(f64(W_ih0)[:, :H].T, 0, "e4m3")
    w_a = mxq(f64(W_ih0)[:, H:].T, 0, "e4m3")
    hq = mxq(f64(h_prev), 1, "e4m3")
    gates = (xq @ w_x) + (aq @ w_a) + f64(b_ih0) + (hq @ mxq(f64(W_hh0).T, 0, "e4m3")) + f64(b_hh0)
    i, f, g, o = np.split(gates, 4, axis=-1)
    c_new = sigmoid(f) * f64(c_prev) + sigmoid(i) * np.tanh(g)
    h_new = sigmoid(o) * np.tanh(c_new)
    return h_new, c_new

@@ -1,0 +1,272 @@
+from contextlib import ExitStack
+
+import concourse.mybir as mybir
+from concourse.masks import make_identity
+
+BF16 = mybir.dt.bfloat16
+F32 = mybir.dt.float32
+U32 = mybir.dt.uint32
+U8 = mybir.dt.uint8
+I32 = mybir.dt.int32
+FP8X4 = mybir.dt.float8_e4m3fn_x4
+ALU = mybir.AluOpType
+FUNC = mybir.ActivationFunctionType
+INNERMOST = mybir.AxisListType.X
+
+P = 128
+PACK = 4
+K_PASS = P * PACK
+B, H, S = 1024, 512, 16
+N_BT = B // P
+N_JC = H // P
+N_GATES = 4
+GATE_I, GATE_F, GATE_G, GATE_O = 0, 1, 2, 3
+N_GC = N_GATES * N_JC
+PAIR = 2
+GATE_SCALE = (0.5, 0.5, 1.0, 0.5)
+
+FLOPS = 2 * B * H * H + 2 * B * (3 * H) * (N_GATES * H)
+
+
+def tile_decoderlstm_pa_t_kernel(
+    tc, x, enc_seq, attn_W, attn_b, h_prev, c_prev, W_ih0, W_hh0, b_ih0, b_hh0, out_0, out_1
+):
+    nc = tc.nc
+    with ExitStack() as ctx:
+        keep = ctx.enter_context(tc.tile_pool(name="keep", bufs=1))
+        stage = ctx.enter_context(tc.tile_pool(name="stage", bufs=3))
+        enc_pool = ctx.enter_context(tc.tile_pool(name="enc", bufs=2))
+        soft_pool = ctx.enter_context(tc.tile_pool(name="soft", bufs=5))
+        prod_pool = ctx.enter_context(tc.tile_pool(name="prod", bufs=3))
+        row_pool = ctx.enter_context(tc.tile_pool(name="row", bufs=2))
+        cell_pool = ctx.enter_context(tc.tile_pool(name="cell", bufs=1))
+        out_pool = ctx.enter_context(tc.tile_pool(name="out", bufs=2))
+        psum_lin = ctx.enter_context(tc.psum_pool(name="psum_lin", bufs=2))
+        psum_gates = ctx.enter_context(tc.psum_pool(name="psum_gates", bufs=2))
+        psum_move = ctx.enter_context(tc.psum_pool(name="psum_move", bufs=4))
+
+        ident_bf = keep.tile([P, P], BF16)
+        make_identity(nc, ident_bf[:])
+        ident_f32 = keep.tile([P, P], F32)
+        make_identity(nc, ident_f32[:])
+
+        bias_rows = keep.tile([P, P], BF16)
+        nc.vector.memset(bias_rows[:].bitcast(I32), 0)
+        nc.sync.dma_start(out=bias_rows[0:N_GC, :], in_=b_ih0.rearrange("(r c) -> r c", c=P))
+        nc.sync.dma_start(out=bias_rows[N_GC : 2 * N_GC, :], in_=b_hh0.rearrange("(r c) -> r c", c=P))
+        nc.sync.dma_start(
+            out=bias_rows[2 * N_GC : 2 * N_GC + N_JC, :], in_=attn_b.rearrange("(r c) -> r c", c=P)
+        )
+        bias_ps = psum_move.tile([P, P], BF16, tag="move")
+        nc.tensor.transpose(bias_ps[:], bias_rows[:], ident_bf[:])
+        bias_cols = keep.tile([P, P], F32)
+        nc.scalar.copy(out=bias_cols[:], in_=bias_ps[:])
+        attn_bias = bias_cols[:, 2 * N_GC : 2 * N_GC + N_JC]
+        gate_bias = keep.tile([P, N_GC], F32)
+        nc.vector.tensor_tensor(
+            out=gate_bias[:], in0=bias_cols[:, 0:N_GC], in1=bias_cols[:, N_GC : 2 * N_GC], op=ALU.add
+        )
+        for gate in range(N_GATES):
+            cols = slice(gate * N_JC, (gate + 1) * N_JC)
+            nc.vector.tensor_scalar_mul(out=gate_bias[:, cols], in0=gate_bias[:, cols], scalar1=GATE_SCALE[gate])
+
+        def operand_tiles(n_chunks, label):
+            words = keep.tile([P, n_chunks, P], U32, name=label + "_words", align_bytes=64)
+            scales = keep.tile([P, n_chunks, P], U8, name=label + "_scales", align_bytes=64)
+            return words, scales
+
+        x_q = operand_tiles(N_BT, "x")
+        h_q = operand_tiles(N_BT, "h")
+        attn_w_q = operand_tiles(N_JC, "attn_w")
+        w_x_q = operand_tiles(N_GC, "w_x")
+        w_att_q = operand_tiles(N_GC, "w_att")
+        w_h_q = operand_tiles(N_GC, "w_h")
+
+        def quantise_256_rows(matrix, k_cols, operand, pair):
+            words, scales = operand
+            rows = matrix[2 * P * pair : 2 * P * (pair + 1), k_cols]
+            raw = stage.tile([P, 2, K_PASS], BF16)
+            nc.sync.dma_start(out=raw[:], in_=rows.rearrange("(a r) k -> r a k", r=P))
+            k_first = psum_move.tile([P, 2, PACK, P], BF16, tag="move")
+            for a in range(2):
+                for t in range(PACK):
+                    nc.tensor.transpose(k_first[:, a, t, :], raw[:, a, t * P : (t + 1) * P], ident_bf[:])
+            grouped = stage.tile([P, 2, P, PACK], BF16, align_bytes=64)
+            nc.scalar.copy(out=grouped[:], in_=k_first[:].rearrange("p a t r -> p a r t"))
+            chunks = slice(2 * pair, 2 * pair + 2)
+            nc.vector.quantize_mx(
+                out=words[:, chunks, :].rearrange("p a r -> p (a r)").bitcast(FP8X4),
+                scales=scales[:, chunks, :].rearrange("p a r -> p (a r)"),
+                in_=grouped[:].rearrange("p a r t -> p (a r t)"),
+            )
+
+        def load_enc(bt):
+            enc_sb = enc_pool.tile([P, S, H], BF16)
+            nc.sync.dma_start(
+                out=enc_sb[:], in_=enc_seq[:, bt * P : (bt + 1) * P, :].rearrange("s b j -> b s j")
+            )
+            return enc_sb
+
+        def attn_lin_in_psum(bt):
+            lin_t_ps = psum_move.tile([P, N_JC, P], F32, tag="move")
+            for jc in range(N_JC):
+                nc.tensor.matmul_mx(
+                    out=lin_t_ps[:, jc, :],
+                    lhsT=attn_w_q[0][:, jc, :].bitcast(FP8X4),
+                    lhsT_scale=attn_w_q[1][:, jc, :],
+                    rhs=x_q[0][:, bt, :].bitcast(FP8X4),
+                    rhs_scale=x_q[1][:, bt, :],
+                    start=True,
+                    stop=True,
+                )
+            lin_t = row_pool.tile([P, N_JC, P], F32)
+            for jc in range(N_JC):
+                nc.scalar.activation(
+                    out=lin_t[:, jc, :], in_=lin_t_ps[:, jc, :], func=FUNC.Identity, bias=attn_bias[:, jc : jc + 1]
+                )
+            lin_ps = psum_lin.tile([P, H], F32)
+            for jc in range(N_JC):
+                nc.tensor.transpose(lin_ps[:, jc * P : (jc + 1) * P], lin_t[:, jc, :], ident_f32[:])
+            return lin_ps
+
+        def softmax_sums(lin_ps, enc_sb, jc, e_sum, enc_e_sum):
+            j_cols = slice(jc * P, (jc + 1) * P)
+            shape = [P, P // PAIR, S, PAIR]
+            enc_v = enc_sb[:, :, j_cols].rearrange("p s (h l) -> p h s l", l=PAIR)
+            lin_v = lin_ps[:, j_cols].rearrange("p (h l) -> p h l", l=PAIR).unsqueeze(2).to_broadcast(shape)
+            e = soft_pool.tile(shape, F32)
+            nc.vector.tensor_tensor(out=e[:], in0=lin_v, in1=enc_v, op=ALU.mult)
+            top = soft_pool.tile([P, P // PAIR, PAIR], F32)
+            nc.vector.tensor_reduce(out=top[:], in_=e[:].rearrange("p h s l -> p h l s"), axis=INNERMOST, op=ALU.max)
+            nc.gpsimd.tensor_tensor(out=e[:], in0=e[:], in1=top[:].unsqueeze(2).to_broadcast(shape), op=ALU.subtract)
+            e_flat = e[:].rearrange("p h s l -> p (h s l)")
+            nc.scalar.activation(out=e_flat, in_=e_flat, func=FUNC.Exp)
+            nc.vector.tensor_reduce(
+                out=e_sum[:, j_cols].rearrange("p (h l) -> p h l", l=PAIR),
+                in_=e[:].rearrange("p h s l -> p h l s"),
+                axis=INNERMOST,
+                op=ALU.add,
+            )
+            enc_e = prod_pool.tile(shape, F32)
+            nc.gpsimd.tensor_tensor(out=enc_e[:], in0=enc_v, in1=e[:], op=ALU.mult)
+            nc.vector.tensor_reduce(
+                out=enc_e_sum[:, j_cols].rearrange("p (h l) -> p h l", l=PAIR),
+                in_=enc_e[:].rearrange("p h s l -> p h l s"),
+                axis=INNERMOST,
+                op=ALU.add,
+            )
+
+        def quantise_attention(e_sum, enc_e_sum):
+            inv_sum = row_pool.tile([P, H], F32)
+            nc.vector.reciprocal(out=inv_sum[:], in_=e_sum[:])
+            attention = row_pool.tile([P, H], F32)
+            nc.vector.tensor_tensor(out=attention[:], in0=enc_e_sum[:], in1=inv_sum[:], op=ALU.mult)
+            att_t_ps = psum_move.tile([P, PACK, P], F32, tag="move")
+            for t in range(PACK):
+                nc.tensor.transpose(att_t_ps[:, t, :], attention[:, t * P : (t + 1) * P], ident_f32[:])
+            att_grouped = row_pool.tile([P, P, PACK], BF16, align_bytes=64)
+            nc.scalar.copy(out=att_grouped[:], in_=att_t_ps[:].rearrange("p t b -> p b t"))
+            att_words = row_pool.tile([P, P], U32, align_bytes=64)
+            att_scales = row_pool.tile([P, P], U8, align_bytes=64)
+            nc.vector.quantize_mx(
+                out=att_words[:].bitcast(FP8X4),
+                scales=att_scales[:],
+                in_=att_grouped[:].rearrange("p b t -> p (b t)"),
+            )
+            return att_words, att_scales
+
+        def lstm_cell(bt, att_words, att_scales):
+            b_rows = slice(bt * P, (bt + 1) * P)
+            c_raw = row_pool.tile([P, H], BF16)
+            nc.sync.dma_start(out=c_raw[:], in_=c_prev[b_rows, :])
+            c_t_ps = psum_move.tile([P, N_JC, P], BF16, tag="move")
+            for jc in range(N_JC):
+                nc.tensor.transpose(c_t_ps[:, jc, :], c_raw[:, jc * P : (jc + 1) * P], ident_bf[:])
+
+            products = (
+                (w_x_q, x_q[0][:, bt, :], x_q[1][:, bt, :]),
+                (w_h_q, h_q[0][:, bt, :], h_q[1][:, bt, :]),
+                (w_att_q, att_words[:], att_scales[:]),
+            )
+            tanh_gate = cell_pool.tile([P, N_JC, N_GATES, P], F32)
+            for jc in range(N_JC):
+                gates_ps = psum_gates.tile([P, N_GATES, P], F32)
+                for gate in range(N_GATES):
+                    gc = gate * N_JC + jc
+                    for i, (weights, v_words, v_scales) in enumerate(products):
+                        nc.tensor.matmul_mx(
+                            out=gates_ps[:, gate, :],
+                            lhsT=weights[0][:, gc, :].bitcast(FP8X4),
+                            lhsT_scale=weights[1][:, gc, :],
+                            rhs=v_words.bitcast(FP8X4),
+                            rhs_scale=v_scales,
+                            start=(i == 0),
+                            stop=(i == len(products) - 1),
+                        )
+                for gate in range(N_GATES):
+                    gc = gate * N_JC + jc
+                    nc.scalar.activation(
+                        out=tanh_gate[:, jc, gate, :],
+                        in_=gates_ps[:, gate, :],
+                        func=FUNC.Tanh,
+                        bias=gate_bias[:, gc : gc + 1],
+                        scale=GATE_SCALE[gate],
+                    )
+
+            kept = cell_pool.tile([P, N_JC, P], F32)
+            nc.vector.scalar_tensor_tensor(
+                out=kept[:], in0=tanh_gate[:, :, GATE_F, :], scalar=1.0, in1=c_t_ps[:], op0=ALU.add, op1=ALU.mult
+            )
+            fresh = cell_pool.tile([P, N_JC, P], F32)
+            nc.vector.scalar_tensor_tensor(
+                out=fresh[:],
+                in0=tanh_gate[:, :, GATE_I, :],
+                scalar=1.0,
+                in1=tanh_gate[:, :, GATE_G, :],
+                op0=ALU.add,
+                op1=ALU.mult,
+            )
+            c_twice = cell_pool.tile([P, N_JC, P], F32)
+            nc.vector.tensor_tensor(out=c_twice[:], in0=kept[:], in1=fresh[:], op=ALU.add)
+            tanh_c = cell_pool.tile([P, N_JC, P], F32)
+            nc.scalar.activation(out=tanh_c[:], in_=c_twice[:], func=FUNC.Tanh, scale=0.5)
+            h_twice = cell_pool.tile([P, N_JC, P], F32)
+            nc.vector.scalar_tensor_tensor(
+                out=h_twice[:], in0=tanh_gate[:, :, GATE_O, :], scalar=1.0, in1=tanh_c[:], op0=ALU.add, op1=ALU.mult
+            )
+            for twice, result_dram in ((h_twice, out_0), (c_twice, out_1)):
+                back_ps = psum_move.tile([P, H], F32, tag="move")
+                for jc in range(N_JC):
+                    nc.tensor.transpose(back_ps[:, jc * P : (jc + 1) * P], twice[:, jc, :], ident_f32[:])
+                result = out_pool.tile([P, H], F32)
+                nc.scalar.mul(out=result[:], in_=back_ps[:], mul=0.5)
+                nc.sync.dma_start(out=result_dram[b_rows, :], in_=result[:])
+
+        first_half = slice(0, H)
+        second_half = slice(H, 2 * H)
+        quantise_256_rows(x, first_half, x_q, 0)
+        for pair in range(N_JC // 2):
+            quantise_256_rows(attn_W, first_half, attn_w_q, pair)
+        enc_next = load_enc(0)
+        lin_next = attn_lin_in_psum(0)
+
+        for bt in range(N_BT):
+            enc_sb, lin_ps = enc_next, lin_next
+            if bt + 1 < N_BT:
+                enc_next = load_enc(bt + 1)
+                lin_next = attn_lin_in_psum(bt + 1)
+            e_sum = row_pool.tile([P, H], F32)
+            enc_e_sum = row_pool.tile([P, H], F32)
+            for jc in range(N_JC):
+                softmax_sums(lin_ps, enc_sb, jc, e_sum, enc_e_sum)
+            if bt == 0:
+                for pair in range(1, N_BT // 2):
+                    quantise_256_rows(x, first_half, x_q, pair)
+                for pair in range(N_BT // 2):
+                    quantise_256_rows(h_prev, first_half, h_q, pair)
+                for pair in range(N_GC // 2):
+                    quantise_256_rows(W_ih0, first_half, w_x_q, pair)
+                    quantise_256_rows(W_hh0, first_half, w_h_q, pair)
+                    quantise_256_rows(W_ih0, second_half, w_att_q, pair)
+            att_words, att_scales = quantise_attention(e_sum, enc_e_sum)
+            lstm_cell(bt, att_words, att_scales)

@@ -24,6 +24,8 @@ GATE_I, GATE_F, GATE_G, GATE_O = 0, 1, 2, 3
 N_GC = N_GATES * N_JC
 PAIR = 2
 GATE_SCALE = (0.5, 0.5, 1.0, 0.5)
+CELL_LAG = 5
+PREP_PER_STEP = 6
 
 FLOPS = 2 * B * H * H + 2 * B * (3 * H) * (N_GATES * H)
 
@@ -34,9 +36,10 @@ def tile_decoderlstm_pa_t_kernel(
     nc = tc.nc
     with ExitStack() as ctx:
         keep = ctx.enter_context(tc.tile_pool(name="keep", bufs=1))
-        stage = ctx.enter_context(tc.tile_pool(name="stage", bufs=3))
+        raw_pool = ctx.enter_context(tc.tile_pool(name="raw", bufs=4))
+        grouped_pool = ctx.enter_context(tc.tile_pool(name="grouped", bufs=PREP_PER_STEP + 2))
         enc_pool = ctx.enter_context(tc.tile_pool(name="enc", bufs=2))
-        soft_pool = ctx.enter_context(tc.tile_pool(name="soft", bufs=5))
+        soft_pool = ctx.enter_context(tc.tile_pool(name="soft", bufs=4))
         prod_pool = ctx.enter_context(tc.tile_pool(name="prod", bufs=3))
         row_pool = ctx.enter_context(tc.tile_pool(name="row", bufs=2))
         cell_pool = ctx.enter_context(tc.tile_pool(name="cell", bufs=1))
@@ -82,17 +85,22 @@ def tile_decoderlstm_pa_t_kernel(
         w_att_q = operand_tiles(N_GC, "w_att")
         w_h_q = operand_tiles(N_GC, "w_h")
 
-        def quantise_256_rows(matrix, k_cols, operand, pair):
-            words, scales = operand
+        def bring_k_to_partitions(item):
+            matrix, k_cols, operand, pair = item
             rows = matrix[2 * P * pair : 2 * P * (pair + 1), k_cols]
-            raw = stage.tile([P, 2, K_PASS], BF16)
+            raw = raw_pool.tile([P, 2, K_PASS], BF16)
             nc.sync.dma_start(out=raw[:], in_=rows.rearrange("(a r) k -> r a k", r=P))
             k_first = psum_move.tile([P, 2, PACK, P], BF16, tag="move")
             for a in range(2):
                 for t in range(PACK):
                     nc.tensor.transpose(k_first[:, a, t, :], raw[:, a, t * P : (t + 1) * P], ident_bf[:])
-            grouped = stage.tile([P, 2, P, PACK], BF16, align_bytes=64)
+            grouped = grouped_pool.tile([P, 2, P, PACK], BF16, align_bytes=64)
             nc.scalar.copy(out=grouped[:], in_=k_first[:].rearrange("p a t r -> p a r t"))
+            return grouped
+
+        def quantise(item, grouped):
+            matrix, k_cols, operand, pair = item
+            words, scales = operand
             chunks = slice(2 * pair, 2 * pair + 2)
             nc.vector.quantize_mx(
                 out=words[:, chunks, :].rearrange("p a r -> p (a r)").bitcast(FP8X4),
@@ -100,14 +108,16 @@ def tile_decoderlstm_pa_t_kernel(
                 in_=grouped[:].rearrange("p a r t -> p (a r t)"),
             )
 
+        enc_of, lin_of, e_of, enc_e_of, sums_of, att_t_of, cell_of = {}, {}, {}, {}, {}, {}, {}
+
         def load_enc(bt):
             enc_sb = enc_pool.tile([P, S, H], BF16)
             nc.sync.dma_start(
                 out=enc_sb[:], in_=enc_seq[:, bt * P : (bt + 1) * P, :].rearrange("s b j -> b s j")
             )
-            return enc_sb
+            enc_of[bt] = enc_sb
 
-        def attn_lin_in_psum(bt):
+        def attn_lin_into_psum(bt):
             lin_t_ps = psum_move.tile([P, N_JC, P], F32, tag="move")
             for jc in range(N_JC):
                 nc.tensor.matmul_mx(
@@ -127,62 +137,82 @@ def tile_decoderlstm_pa_t_kernel(
             lin_ps = psum_lin.tile([P, H], F32)
             for jc in range(N_JC):
                 nc.tensor.transpose(lin_ps[:, jc * P : (jc + 1) * P], lin_t[:, jc, :], ident_f32[:])
-            return lin_ps
+            lin_of[bt] = lin_ps
 
-        def softmax_sums(lin_ps, enc_sb, jc, e_sum, enc_e_sum):
-            j_cols = slice(jc * P, (jc + 1) * P)
-            shape = [P, P // PAIR, S, PAIR]
-            enc_v = enc_sb[:, :, j_cols].rearrange("p s (h l) -> p h s l", l=PAIR)
-            lin_v = lin_ps[:, j_cols].rearrange("p (h l) -> p h l", l=PAIR).unsqueeze(2).to_broadcast(shape)
-            e = soft_pool.tile(shape, F32)
-            nc.vector.tensor_tensor(out=e[:], in0=lin_v, in1=enc_v, op=ALU.mult)
+        soft_shape = [P, P // PAIR, S, PAIR]
+
+        def enc_view(c):
+            bt, jc = divmod(c, N_JC)
+            return enc_of[bt][:, :, jc * P : (jc + 1) * P].rearrange("p s (h l) -> p h s l", l=PAIR)
+
+        def over_s(tile_ap):
+            return tile_ap.rearrange("p h s l -> p h l s")
+
+        def pairs(row_ap):
+            return row_ap.rearrange("p (h l) -> p h l", l=PAIR)
+
+        def exp_of_shifted_scores(c):
+            bt, jc = divmod(c, N_JC)
+            lin_v = pairs(lin_of[bt][:, jc * P : (jc + 1) * P]).unsqueeze(2).to_broadcast(soft_shape)
+            e = soft_pool.tile(soft_shape, F32)
+            nc.vector.tensor_tensor(out=e[:], in0=lin_v, in1=enc_view(c), op=ALU.mult)
             top = soft_pool.tile([P, P // PAIR, PAIR], F32)
-            nc.vector.tensor_reduce(out=top[:], in_=e[:].rearrange("p h s l -> p h l s"), axis=INNERMOST, op=ALU.max)
-            nc.gpsimd.tensor_tensor(out=e[:], in0=e[:], in1=top[:].unsqueeze(2).to_broadcast(shape), op=ALU.subtract)
+            nc.vector.tensor_reduce(out=top[:], in_=over_s(e[:]), axis=INNERMOST, op=ALU.max)
+            nc.gpsimd.tensor_tensor(
+                out=e[:], in0=e[:], in1=top[:].unsqueeze(2).to_broadcast(soft_shape), op=ALU.subtract
+            )
             e_flat = e[:].rearrange("p h s l -> p (h s l)")
             nc.scalar.activation(out=e_flat, in_=e_flat, func=FUNC.Exp)
-            nc.vector.tensor_reduce(
-                out=e_sum[:, j_cols].rearrange("p (h l) -> p h l", l=PAIR),
-                in_=e[:].rearrange("p h s l -> p h l s"),
-                axis=INNERMOST,
-                op=ALU.add,
-            )
-            enc_e = prod_pool.tile(shape, F32)
-            nc.gpsimd.tensor_tensor(out=enc_e[:], in0=enc_v, in1=e[:], op=ALU.mult)
-            nc.vector.tensor_reduce(
-                out=enc_e_sum[:, j_cols].rearrange("p (h l) -> p h l", l=PAIR),
-                in_=enc_e[:].rearrange("p h s l -> p h l s"),
-                axis=INNERMOST,
-                op=ALU.add,
-            )
+            e_of[c] = e
 
-        def quantise_attention(e_sum, enc_e_sum):
-            inv_sum = row_pool.tile([P, H], F32)
-            nc.vector.reciprocal(out=inv_sum[:], in_=e_sum[:])
-            attention = row_pool.tile([P, H], F32)
-            nc.vector.tensor_tensor(out=attention[:], in0=enc_e_sum[:], in1=inv_sum[:], op=ALU.mult)
-            att_t_ps = psum_move.tile([P, PACK, P], F32, tag="move")
-            for t in range(PACK):
-                nc.tensor.transpose(att_t_ps[:, t, :], attention[:, t * P : (t + 1) * P], ident_f32[:])
+        def sum_e_and_weigh_enc(c):
+            bt, jc = divmod(c, N_JC)
+            if jc == 0:
+                e_sum = row_pool.tile([P, H], F32)
+                enc_e_sum = row_pool.tile([P, H], F32)
+                sums_of[bt] = (e_sum, enc_e_sum)
+            e_sum = sums_of[bt][0]
+            nc.vector.tensor_reduce(
+                out=pairs(e_sum[:, jc * P : (jc + 1) * P]), in_=over_s(e_of[c][:]), axis=INNERMOST, op=ALU.add
+            )
+            enc_e = prod_pool.tile(soft_shape, F32)
+            nc.gpsimd.tensor_tensor(out=enc_e[:], in0=enc_view(c), in1=e_of[c][:], op=ALU.mult)
+            enc_e_of[c] = enc_e
+
+        def attention_of(c):
+            bt, jc = divmod(c, N_JC)
+            j_cols = slice(jc * P, (jc + 1) * P)
+            e_sum, enc_e_sum = sums_of[bt]
+            nc.vector.tensor_reduce(
+                out=pairs(enc_e_sum[:, j_cols]), in_=over_s(enc_e_of[c][:]), axis=INNERMOST, op=ALU.add
+            )
+            nc.vector.reciprocal(out=e_sum[:, j_cols], in_=e_sum[:, j_cols])
+            attention = soft_pool.tile([P, P], F32)
+            nc.vector.tensor_tensor(out=attention[:], in0=enc_e_sum[:, j_cols], in1=e_sum[:, j_cols], op=ALU.mult)
+            if jc == 0:
+                att_t_ps = psum_move.tile([P, PACK, P], F32, tag="move")
+                att_t_of[bt] = att_t_ps
+            nc.tensor.transpose(att_t_of[bt][:, jc, :], attention[:], ident_f32[:])
+
+        def cell_stage_0(bt):
             att_grouped = row_pool.tile([P, P, PACK], BF16, align_bytes=64)
-            nc.scalar.copy(out=att_grouped[:], in_=att_t_ps[:].rearrange("p t b -> p b t"))
+            nc.scalar.copy(out=att_grouped[:], in_=att_t_of[bt][:].rearrange("p t b -> p b t"))
+            c_raw = row_pool.tile([P, H], BF16)
+            nc.sync.dma_start(out=c_raw[:], in_=c_prev[bt * P : (bt + 1) * P, :])
+            cell_of[bt, "att_grouped"] = att_grouped
+            cell_of[bt, "c_raw"] = c_raw
+
+        def cell_stage_1(bt):
             att_words = row_pool.tile([P, P], U32, align_bytes=64)
             att_scales = row_pool.tile([P, P], U8, align_bytes=64)
             nc.vector.quantize_mx(
                 out=att_words[:].bitcast(FP8X4),
                 scales=att_scales[:],
-                in_=att_grouped[:].rearrange("p b t -> p (b t)"),
+                in_=cell_of[bt, "att_grouped"][:].rearrange("p b t -> p (b t)"),
             )
-            return att_words, att_scales
-
-        def lstm_cell(bt, att_words, att_scales):
-            b_rows = slice(bt * P, (bt + 1) * P)
-            c_raw = row_pool.tile([P, H], BF16)
-            nc.sync.dma_start(out=c_raw[:], in_=c_prev[b_rows, :])
             c_t_ps = psum_move.tile([P, N_JC, P], BF16, tag="move")
             for jc in range(N_JC):
-                nc.tensor.transpose(c_t_ps[:, jc, :], c_raw[:, jc * P : (jc + 1) * P], ident_bf[:])
-
+                nc.tensor.transpose(c_t_ps[:, jc, :], cell_of[bt, "c_raw"][:, jc * P : (jc + 1) * P], ident_bf[:])
             products = (
                 (w_x_q, x_q[0][:, bt, :], x_q[1][:, bt, :]),
                 (w_h_q, h_q[0][:, bt, :], h_q[1][:, bt, :]),
@@ -212,10 +242,27 @@ def tile_decoderlstm_pa_t_kernel(
                         bias=gate_bias[:, gc : gc + 1],
                         scale=GATE_SCALE[gate],
                     )
+            cell_of[bt, "c_t_ps"] = c_t_ps
+            cell_of[bt, "tanh_gate"] = tanh_gate
 
+        def store_half_of(twice, result_dram, bt):
+            back_ps = psum_move.tile([P, H], F32, tag="move")
+            for jc in range(N_JC):
+                nc.tensor.transpose(back_ps[:, jc * P : (jc + 1) * P], twice[:, jc, :], ident_f32[:])
+            result = out_pool.tile([P, H], F32)
+            nc.scalar.mul(out=result[:], in_=back_ps[:], mul=0.5)
+            nc.sync.dma_start(out=result_dram[bt * P : (bt + 1) * P, :], in_=result[:])
+
+        def cell_stage_2(bt):
+            tanh_gate = cell_of[bt, "tanh_gate"]
             kept = cell_pool.tile([P, N_JC, P], F32)
             nc.vector.scalar_tensor_tensor(
-                out=kept[:], in0=tanh_gate[:, :, GATE_F, :], scalar=1.0, in1=c_t_ps[:], op0=ALU.add, op1=ALU.mult
+                out=kept[:],
+                in0=tanh_gate[:, :, GATE_F, :],
+                scalar=1.0,
+                in1=cell_of[bt, "c_t_ps"][:],
+                op0=ALU.add,
+                op1=ALU.mult,
             )
             fresh = cell_pool.tile([P, N_JC, P], F32)
             nc.vector.scalar_tensor_tensor(
@@ -230,43 +277,66 @@ def tile_decoderlstm_pa_t_kernel(
             nc.vector.tensor_tensor(out=c_twice[:], in0=kept[:], in1=fresh[:], op=ALU.add)
             tanh_c = cell_pool.tile([P, N_JC, P], F32)
             nc.scalar.activation(out=tanh_c[:], in_=c_twice[:], func=FUNC.Tanh, scale=0.5)
+            store_half_of(c_twice, out_1, bt)
+            cell_of[bt, "tanh_c"] = tanh_c
+
+        def cell_stage_3(bt):
             h_twice = cell_pool.tile([P, N_JC, P], F32)
             nc.vector.scalar_tensor_tensor(
-                out=h_twice[:], in0=tanh_gate[:, :, GATE_O, :], scalar=1.0, in1=tanh_c[:], op0=ALU.add, op1=ALU.mult
+                out=h_twice[:],
+                in0=cell_of[bt, "tanh_gate"][:, :, GATE_O, :],
+                scalar=1.0,
+                in1=cell_of[bt, "tanh_c"][:],
+                op0=ALU.add,
+                op1=ALU.mult,
             )
-            for twice, result_dram in ((h_twice, out_0), (c_twice, out_1)):
-                back_ps = psum_move.tile([P, H], F32, tag="move")
-                for jc in range(N_JC):
-                    nc.tensor.transpose(back_ps[:, jc * P : (jc + 1) * P], twice[:, jc, :], ident_f32[:])
-                result = out_pool.tile([P, H], F32)
-                nc.scalar.mul(out=result[:], in_=back_ps[:], mul=0.5)
-                nc.sync.dma_start(out=result_dram[b_rows, :], in_=result[:])
+            store_half_of(h_twice, out_0, bt)
 
         first_half = slice(0, H)
         second_half = slice(H, 2 * H)
-        quantise_256_rows(x, first_half, x_q, 0)
-        for pair in range(N_JC // 2):
-            quantise_256_rows(attn_W, first_half, attn_w_q, pair)
-        enc_next = load_enc(0)
-        lin_next = attn_lin_in_psum(0)
+        first = [(x, first_half, x_q, 0)] + [(attn_W, first_half, attn_w_q, pair) for pair in range(N_JC // 2)]
+        later = [(x, first_half, x_q, pair) for pair in range(1, N_BT // 2)]
+        later += [(h_prev, first_half, h_q, pair) for pair in range(N_BT // 2)]
+        for pair in range(N_GC // 2):
+            later += [
+                (W_ih0, first_half, w_x_q, pair),
+                (W_hh0, first_half, w_h_q, pair),
+                (W_ih0, second_half, w_att_q, pair),
+            ]
+        later_grouped = []
 
-        for bt in range(N_BT):
-            enc_sb, lin_ps = enc_next, lin_next
-            if bt + 1 < N_BT:
-                enc_next = load_enc(bt + 1)
-                lin_next = attn_lin_in_psum(bt + 1)
-            e_sum = row_pool.tile([P, H], F32)
-            enc_e_sum = row_pool.tile([P, H], F32)
-            for jc in range(N_JC):
-                softmax_sums(lin_ps, enc_sb, jc, e_sum, enc_e_sum)
-            if bt == 0:
-                for pair in range(1, N_BT // 2):
-                    quantise_256_rows(x, first_half, x_q, pair)
-                for pair in range(N_BT // 2):
-                    quantise_256_rows(h_prev, first_half, h_q, pair)
-                for pair in range(N_GC // 2):
-                    quantise_256_rows(W_ih0, first_half, w_x_q, pair)
-                    quantise_256_rows(W_hh0, first_half, w_h_q, pair)
-                    quantise_256_rows(W_ih0, second_half, w_att_q, pair)
-            att_words, att_scales = quantise_attention(e_sum, enc_e_sum)
-            lstm_cell(bt, att_words, att_scales)
+        def share_of(step):
+            return range(min(step * PREP_PER_STEP, len(later)), min((step + 1) * PREP_PER_STEP, len(later)))
+
+        with tc.manual_schedule():
+            for item in first:
+                quantise(item, bring_k_to_partitions(item))
+            load_enc(0)
+            attn_lin_into_psum(0)
+
+            n_chunks = N_BT * N_JC
+            for step in range(n_chunks + CELL_LAG + 4):
+                if step < n_chunks:
+                    exp_of_shifted_scores(step)
+                if 0 <= step - 1 < n_chunks:
+                    sum_e_and_weigh_enc(step - 1)
+                if 0 <= step - 2 < n_chunks:
+                    attention_of(step - 2)
+                if step >= 1:
+                    for n in share_of(step - 1):
+                        quantise(later[n], later_grouped[n])
+                bt, cell_stage = divmod(step - CELL_LAG, 4)
+                if 0 <= bt < N_BT:
+                    if cell_stage == 0:
+                        cell_stage_0(bt)
+                    if cell_stage == 1:
+                        cell_stage_1(bt)
+                    if cell_stage == 2:
+                        cell_stage_2(bt)
+                    if cell_stage == 3:
+                        cell_stage_3(bt)
+                if step % N_JC == 1 and step // N_JC + 1 < N_BT:
+                    load_enc(step // N_JC + 1)
+                    attn_lin_into_psum(step // N_JC + 1)
+                for n in share_of(step):
+                    later_grouped.append(bring_k_to_partitions(later[n]))

@@ -11,7 +11,7 @@ I32 = mybir.dt.int32
 FP8X4 = mybir.dt.float8_e4m3fn_x4
 ALU = mybir.AluOpType
 FUNC = mybir.ActivationFunctionType
-INNERMOST = mybir.AxisListType.X
+INNER_TWO = mybir.AxisListType.XY
 
 P = 128
 PACK = 4
@@ -22,7 +22,8 @@ N_JC = H // P
 N_GATES = 4
 GATE_I, GATE_F, GATE_G, GATE_O = 0, 1, 2, 3
 N_GC = N_GATES * N_JC
-PAIR = 2
+S_RUN = 4
+S_OUT = S // S_RUN
 GATE_SCALE = (0.5, 0.5, 1.0, 0.5)
 CELL_LAG = 5
 PREP_PER_STEP = 6
@@ -39,6 +40,7 @@ def tile_decoderlstm_pa_t_kernel(
         raw_pool = ctx.enter_context(tc.tile_pool(name="raw", bufs=4))
         grouped_pool = ctx.enter_context(tc.tile_pool(name="grouped", bufs=PREP_PER_STEP + 2))
         enc_pool = ctx.enter_context(tc.tile_pool(name="enc", bufs=2))
+        enc_r_pool = ctx.enter_context(tc.tile_pool(name="enc_r", bufs=4))
         soft_pool = ctx.enter_context(tc.tile_pool(name="soft", bufs=4))
         prod_pool = ctx.enter_context(tc.tile_pool(name="prod", bufs=3))
         row_pool = ctx.enter_context(tc.tile_pool(name="row", bufs=2))
@@ -108,7 +110,7 @@ def tile_decoderlstm_pa_t_kernel(
                 in_=grouped[:].rearrange("p a r t -> p (a r t)"),
             )
 
-        enc_of, lin_of, e_of, enc_e_of, sums_of, att_t_of, cell_of = {}, {}, {}, {}, {}, {}, {}
+        enc_of, enc_r_of, lin_of, e_of, enc_e_of, sums_of, att_t_of, cell_of = {}, {}, {}, {}, {}, {}, {}, {}
 
         def load_enc(bt):
             enc_sb = enc_pool.tile([P, S, H], BF16)
@@ -139,29 +141,33 @@ def tile_decoderlstm_pa_t_kernel(
                 nc.tensor.transpose(lin_ps[:, jc * P : (jc + 1) * P], lin_t[:, jc, :], ident_f32[:])
             lin_of[bt] = lin_ps
 
-        soft_shape = [P, P // PAIR, S, PAIR]
+        soft_shape = [P, S_OUT, P, S_RUN]
 
-        def enc_view(c):
+        def regroup_enc(c):
             bt, jc = divmod(c, N_JC)
-            return enc_of[bt][:, :, jc * P : (jc + 1) * P].rearrange("p s (h l) -> p h s l", l=PAIR)
+            enc_r = enc_r_pool.tile(soft_shape, BF16)
+            nc.scalar.copy(
+                out=enc_r[:],
+                in_=enc_of[bt][:, :, jc * P : (jc + 1) * P].rearrange("p (o r) j -> p o j r", r=S_RUN),
+            )
+            enc_r_of[c] = enc_r
 
         def over_s(tile_ap):
-            return tile_ap.rearrange("p h s l -> p h l s")
+            return tile_ap.rearrange("p o j r -> p j o r")
 
-        def pairs(row_ap):
-            return row_ap.rearrange("p (h l) -> p h l", l=PAIR)
+        def for_all_s(row_ap):
+            return row_ap.unsqueeze(1).unsqueeze(3).to_broadcast(soft_shape)
 
         def exp_of_shifted_scores(c):
             bt, jc = divmod(c, N_JC)
-            lin_v = pairs(lin_of[bt][:, jc * P : (jc + 1) * P]).unsqueeze(2).to_broadcast(soft_shape)
             e = soft_pool.tile(soft_shape, F32)
-            nc.vector.tensor_tensor(out=e[:], in0=lin_v, in1=enc_view(c), op=ALU.mult)
-            top = soft_pool.tile([P, P // PAIR, PAIR], F32)
-            nc.vector.tensor_reduce(out=top[:], in_=over_s(e[:]), axis=INNERMOST, op=ALU.max)
-            nc.gpsimd.tensor_tensor(
-                out=e[:], in0=e[:], in1=top[:].unsqueeze(2).to_broadcast(soft_shape), op=ALU.subtract
+            nc.vector.tensor_tensor(
+                out=e[:], in0=for_all_s(lin_of[bt][:, jc * P : (jc + 1) * P]), in1=enc_r_of[c][:], op=ALU.mult
             )
-            e_flat = e[:].rearrange("p h s l -> p (h s l)")
+            top = soft_pool.tile([P, P], F32)
+            nc.vector.tensor_reduce(out=top[:], in_=over_s(e[:]), axis=INNER_TWO, op=ALU.max)
+            nc.gpsimd.tensor_tensor(out=e[:], in0=e[:], in1=for_all_s(top[:]), op=ALU.subtract)
+            e_flat = e[:].rearrange("p o j r -> p (o j r)")
             nc.scalar.activation(out=e_flat, in_=e_flat, func=FUNC.Exp)
             e_of[c] = e
 
@@ -173,19 +179,17 @@ def tile_decoderlstm_pa_t_kernel(
                 sums_of[bt] = (e_sum, enc_e_sum)
             e_sum = sums_of[bt][0]
             nc.vector.tensor_reduce(
-                out=pairs(e_sum[:, jc * P : (jc + 1) * P]), in_=over_s(e_of[c][:]), axis=INNERMOST, op=ALU.add
+                out=e_sum[:, jc * P : (jc + 1) * P], in_=over_s(e_of[c][:]), axis=INNER_TWO, op=ALU.add
             )
             enc_e = prod_pool.tile(soft_shape, F32)
-            nc.gpsimd.tensor_tensor(out=enc_e[:], in0=enc_view(c), in1=e_of[c][:], op=ALU.mult)
+            nc.gpsimd.tensor_tensor(out=enc_e[:], in0=enc_r_of[c][:], in1=e_of[c][:], op=ALU.mult)
             enc_e_of[c] = enc_e
 
         def attention_of(c):
             bt, jc = divmod(c, N_JC)
             j_cols = slice(jc * P, (jc + 1) * P)
             e_sum, enc_e_sum = sums_of[bt]
-            nc.vector.tensor_reduce(
-                out=pairs(enc_e_sum[:, j_cols]), in_=over_s(enc_e_of[c][:]), axis=INNERMOST, op=ALU.add
-            )
+            nc.vector.tensor_reduce(out=enc_e_sum[:, j_cols], in_=over_s(enc_e_of[c][:]), axis=INNER_TWO, op=ALU.add)
             nc.vector.reciprocal(out=e_sum[:, j_cols], in_=e_sum[:, j_cols])
             attention = soft_pool.tile([P, P], F32)
             nc.vector.tensor_tensor(out=attention[:], in0=enc_e_sum[:, j_cols], in1=e_sum[:, j_cols], op=ALU.mult)
@@ -313,9 +317,12 @@ def tile_decoderlstm_pa_t_kernel(
                 quantise(item, bring_k_to_partitions(item))
             load_enc(0)
             attn_lin_into_psum(0)
+            regroup_enc(0)
 
             n_chunks = N_BT * N_JC
             for step in range(n_chunks + CELL_LAG + 4):
+                if step + 1 < n_chunks:
+                    regroup_enc(step + 1)
                 if step < n_chunks:
                     exp_of_shifted_scores(step)
                 if 0 <= step - 1 < n_chunks:

@@ -158,18 +158,21 @@ def tile_decoderlstm_pa_t_kernel(
         def for_all_s(row_ap):
             return row_ap.unsqueeze(1).unsqueeze(3).to_broadcast(soft_shape)
 
-        def exp_of_shifted_scores(c):
+        def scores(c):
             bt, jc = divmod(c, N_JC)
             e = soft_pool.tile(soft_shape, F32)
             nc.vector.tensor_tensor(
                 out=e[:], in0=for_all_s(lin_of[bt][:, jc * P : (jc + 1) * P]), in1=enc_r_of[c][:], op=ALU.mult
             )
+            e_of[c] = e
+
+        def exp_of_shifted_scores(c):
+            e = e_of[c]
             top = soft_pool.tile([P, P], F32)
             nc.vector.tensor_reduce(out=top[:], in_=over_s(e[:]), axis=INNER_TWO, op=ALU.max)
             nc.gpsimd.tensor_tensor(out=e[:], in0=e[:], in1=for_all_s(top[:]), op=ALU.subtract)
             e_flat = e[:].rearrange("p o j r -> p (o j r)")
             nc.scalar.activation(out=e_flat, in_=e_flat, func=FUNC.Exp)
-            e_of[c] = e
 
         def sum_e_and_weigh_enc(c):
             bt, jc = divmod(c, N_JC)
@@ -192,7 +195,7 @@ def tile_decoderlstm_pa_t_kernel(
             nc.vector.tensor_reduce(out=enc_e_sum[:, j_cols], in_=over_s(enc_e_of[c][:]), axis=INNER_TWO, op=ALU.add)
             nc.vector.reciprocal(out=e_sum[:, j_cols], in_=e_sum[:, j_cols])
             attention = soft_pool.tile([P, P], F32)
-            nc.vector.tensor_tensor(out=attention[:], in0=enc_e_sum[:, j_cols], in1=e_sum[:, j_cols], op=ALU.mult)
+            nc.gpsimd.tensor_tensor(out=attention[:], in0=enc_e_sum[:, j_cols], in1=e_sum[:, j_cols], op=ALU.mult)
             if jc == 0:
                 att_t_ps = psum_move.tile([P, PACK, P], F32, tag="move")
                 att_t_of[bt] = att_t_ps
@@ -206,7 +209,7 @@ def tile_decoderlstm_pa_t_kernel(
             cell_of[bt, "att_grouped"] = att_grouped
             cell_of[bt, "c_raw"] = c_raw
 
-        def cell_stage_1(bt):
+        def quantise_attention(bt):
             att_words = row_pool.tile([P, P], U32, align_bytes=64)
             att_scales = row_pool.tile([P, P], U8, align_bytes=64)
             nc.vector.quantize_mx(
@@ -214,6 +217,10 @@ def tile_decoderlstm_pa_t_kernel(
                 scales=att_scales[:],
                 in_=cell_of[bt, "att_grouped"][:].rearrange("p b t -> p (b t)"),
             )
+            cell_of[bt, "att_q"] = (att_words, att_scales)
+
+        def cell_stage_1(bt):
+            att_words, att_scales = cell_of[bt, "att_q"]
             c_t_ps = psum_move.tile([P, N_JC, P], BF16, tag="move")
             for jc in range(N_JC):
                 nc.tensor.transpose(c_t_ps[:, jc, :], cell_of[bt, "c_raw"][:, jc * P : (jc + 1) * P], ident_bf[:])
@@ -246,6 +253,8 @@ def tile_decoderlstm_pa_t_kernel(
                         bias=gate_bias[:, gc : gc + 1],
                         scale=GATE_SCALE[gate],
                     )
+            for gate in (GATE_I, GATE_O):
+                nc.scalar.add(out=tanh_gate[:, :, gate, :], in_=tanh_gate[:, :, gate, :], add=1.0)
             cell_of[bt, "c_t_ps"] = c_t_ps
             cell_of[bt, "tanh_gate"] = tanh_gate
 
@@ -269,16 +278,11 @@ def tile_decoderlstm_pa_t_kernel(
                 op1=ALU.mult,
             )
             fresh = cell_pool.tile([P, N_JC, P], F32)
-            nc.vector.scalar_tensor_tensor(
-                out=fresh[:],
-                in0=tanh_gate[:, :, GATE_I, :],
-                scalar=1.0,
-                in1=tanh_gate[:, :, GATE_G, :],
-                op0=ALU.add,
-                op1=ALU.mult,
+            nc.gpsimd.tensor_tensor(
+                out=fresh[:], in0=tanh_gate[:, :, GATE_I, :], in1=tanh_gate[:, :, GATE_G, :], op=ALU.mult
             )
             c_twice = cell_pool.tile([P, N_JC, P], F32)
-            nc.vector.tensor_tensor(out=c_twice[:], in0=kept[:], in1=fresh[:], op=ALU.add)
+            nc.gpsimd.tensor_tensor(out=c_twice[:], in0=kept[:], in1=fresh[:], op=ALU.add)
             tanh_c = cell_pool.tile([P, N_JC, P], F32)
             nc.scalar.activation(out=tanh_c[:], in_=c_twice[:], func=FUNC.Tanh, scale=0.5)
             store_half_of(c_twice, out_1, bt)
@@ -286,13 +290,8 @@ def tile_decoderlstm_pa_t_kernel(
 
         def cell_stage_3(bt):
             h_twice = cell_pool.tile([P, N_JC, P], F32)
-            nc.vector.scalar_tensor_tensor(
-                out=h_twice[:],
-                in0=cell_of[bt, "tanh_gate"][:, :, GATE_O, :],
-                scalar=1.0,
-                in1=cell_of[bt, "tanh_c"][:],
-                op0=ALU.add,
-                op1=ALU.mult,
+            nc.gpsimd.tensor_tensor(
+                out=h_twice[:], in0=cell_of[bt, "tanh_gate"][:, :, GATE_O, :], in1=cell_of[bt, "tanh_c"][:], op=ALU.mult
             )
             store_half_of(h_twice, out_0, bt)
 
@@ -323,16 +322,20 @@ def tile_decoderlstm_pa_t_kernel(
             for step in range(n_chunks + CELL_LAG + 4):
                 if step + 1 < n_chunks:
                     regroup_enc(step + 1)
+                bt, cell_stage = divmod(step - CELL_LAG, 4)
+                if step < n_chunks:
+                    scores(step)
+                if step >= 1:
+                    for n in share_of(step - 1):
+                        quantise(later[n], later_grouped[n])
+                if 0 <= bt < N_BT and cell_stage == 1:
+                    quantise_attention(bt)
                 if step < n_chunks:
                     exp_of_shifted_scores(step)
                 if 0 <= step - 1 < n_chunks:
                     sum_e_and_weigh_enc(step - 1)
                 if 0 <= step - 2 < n_chunks:
                     attention_of(step - 2)
-                if step >= 1:
-                    for n in share_of(step - 1):
-                        quantise(later[n], later_grouped[n])
-                bt, cell_stage = divmod(step - CELL_LAG, 4)
                 if 0 <= bt < N_BT:
                     if cell_stage == 0:
                         cell_stage_0(bt)

@@ -19,13 +19,13 @@ K_PASS = P * PACK
 B, H, S = 1024, 512, 16
 N_BT = B // P
 N_JC = H // P
+N_CHUNKS = N_BT * N_JC
 N_GATES = 4
 GATE_I, GATE_F, GATE_G, GATE_O = 0, 1, 2, 3
 N_GC = N_GATES * N_JC
 S_RUN = 4
 S_OUT = S // S_RUN
 GATE_SCALE = (0.5, 0.5, 1.0, 0.5)
-CELL_LAG = 5
 PREP_PER_STEP = 6
 
 FLOPS = 2 * B * H * H + 2 * B * (3 * H) * (N_GATES * H)
@@ -40,7 +40,6 @@ def tile_decoderlstm_pa_t_kernel(
         raw_pool = ctx.enter_context(tc.tile_pool(name="raw", bufs=4))
         grouped_pool = ctx.enter_context(tc.tile_pool(name="grouped", bufs=PREP_PER_STEP + 2))
         enc_pool = ctx.enter_context(tc.tile_pool(name="enc", bufs=2))
-        enc_r_pool = ctx.enter_context(tc.tile_pool(name="enc_r", bufs=4))
         soft_pool = ctx.enter_context(tc.tile_pool(name="soft", bufs=4))
         prod_pool = ctx.enter_context(tc.tile_pool(name="prod", bufs=3))
         row_pool = ctx.enter_context(tc.tile_pool(name="row", bufs=2))
@@ -87,8 +86,8 @@ def tile_decoderlstm_pa_t_kernel(
         w_att_q = operand_tiles(N_GC, "w_att")
         w_h_q = operand_tiles(N_GC, "w_h")
 
-        def bring_k_to_partitions(item):
-            matrix, k_cols, operand, pair = item
+        def bring_k_to_partitions(block):
+            matrix, k_cols, operand, pair = block
             rows = matrix[2 * P * pair : 2 * P * (pair + 1), k_cols]
             raw = raw_pool.tile([P, 2, K_PASS], BF16)
             nc.sync.dma_start(out=raw[:], in_=rows.rearrange("(a r) k -> r a k", r=P))
@@ -100,8 +99,8 @@ def tile_decoderlstm_pa_t_kernel(
             nc.scalar.copy(out=grouped[:], in_=k_first[:].rearrange("p a t r -> p a r t"))
             return grouped
 
-        def quantise(item, grouped):
-            matrix, k_cols, operand, pair = item
+        def quantise(block, grouped):
+            matrix, k_cols, operand, pair = block
             words, scales = operand
             chunks = slice(2 * pair, 2 * pair + 2)
             nc.vector.quantize_mx(
@@ -110,7 +109,8 @@ def tile_decoderlstm_pa_t_kernel(
                 in_=grouped[:].rearrange("p a r t -> p (a r t)"),
             )
 
-        enc_of, enc_r_of, lin_of, e_of, enc_e_of, sums_of, att_t_of, cell_of = {}, {}, {}, {}, {}, {}, {}, {}
+        enc_of, enc_r_of, lin_of, e_of, top_of, enc_e_of = {}, {}, {}, {}, {}, {}
+        e_sum_of, enc_e_sum_of, cell_of = {}, {}, {}
 
         def load_enc(bt):
             enc_sb = enc_pool.tile([P, S, H], BF16)
@@ -143,20 +143,20 @@ def tile_decoderlstm_pa_t_kernel(
 
         soft_shape = [P, S_OUT, P, S_RUN]
 
-        def regroup_enc(c):
-            bt, jc = divmod(c, N_JC)
-            enc_r = enc_r_pool.tile(soft_shape, BF16)
-            nc.scalar.copy(
-                out=enc_r[:],
-                in_=enc_of[bt][:, :, jc * P : (jc + 1) * P].rearrange("p (o r) j -> p o j r", r=S_RUN),
-            )
-            enc_r_of[c] = enc_r
-
         def over_s(tile_ap):
             return tile_ap.rearrange("p o j r -> p j o r")
 
         def for_all_s(row_ap):
             return row_ap.unsqueeze(1).unsqueeze(3).to_broadcast(soft_shape)
+
+        def regroup_enc(c):
+            bt, jc = divmod(c, N_JC)
+            enc_r = soft_pool.tile(soft_shape, BF16)
+            nc.scalar.copy(
+                out=enc_r[:],
+                in_=enc_of[bt][:, :, jc * P : (jc + 1) * P].rearrange("p (o r) j -> p o j r", r=S_RUN),
+            )
+            enc_r_of[c] = enc_r
 
         def scores(c):
             bt, jc = divmod(c, N_JC)
@@ -166,47 +166,58 @@ def tile_decoderlstm_pa_t_kernel(
             )
             e_of[c] = e
 
-        def exp_of_shifted_scores(c):
-            e = e_of[c]
+        def max_over_s(c):
             top = soft_pool.tile([P, P], F32)
-            nc.vector.tensor_reduce(out=top[:], in_=over_s(e[:]), axis=INNER_TWO, op=ALU.max)
-            nc.gpsimd.tensor_tensor(out=e[:], in0=e[:], in1=for_all_s(top[:]), op=ALU.subtract)
-            e_flat = e[:].rearrange("p o j r -> p (o j r)")
+            nc.vector.tensor_reduce(out=top[:], in_=over_s(e_of[c][:]), axis=INNER_TWO, op=ALU.max)
+            top_of[c] = top
+
+        def subtract_max(c):
+            nc.gpsimd.tensor_tensor(out=e_of[c][:], in0=e_of[c][:], in1=for_all_s(top_of[c][:]), op=ALU.subtract)
+
+        def exponential(c):
+            e_flat = e_of[c][:].rearrange("p o j r -> p (o j r)")
             nc.scalar.activation(out=e_flat, in_=e_flat, func=FUNC.Exp)
 
-        def sum_e_and_weigh_enc(c):
-            bt, jc = divmod(c, N_JC)
-            if jc == 0:
-                e_sum = row_pool.tile([P, H], F32)
-                enc_e_sum = row_pool.tile([P, H], F32)
-                sums_of[bt] = (e_sum, enc_e_sum)
-            e_sum = sums_of[bt][0]
-            nc.vector.tensor_reduce(
-                out=e_sum[:, jc * P : (jc + 1) * P], in_=over_s(e_of[c][:]), axis=INNER_TWO, op=ALU.add
-            )
+        def weigh_enc(c):
             enc_e = prod_pool.tile(soft_shape, F32)
             nc.gpsimd.tensor_tensor(out=enc_e[:], in0=enc_r_of[c][:], in1=e_of[c][:], op=ALU.mult)
             enc_e_of[c] = enc_e
 
-        def attention_of(c):
+        def sum_e(c):
             bt, jc = divmod(c, N_JC)
-            j_cols = slice(jc * P, (jc + 1) * P)
-            e_sum, enc_e_sum = sums_of[bt]
-            nc.vector.tensor_reduce(out=enc_e_sum[:, j_cols], in_=over_s(enc_e_of[c][:]), axis=INNER_TWO, op=ALU.add)
-            nc.vector.reciprocal(out=e_sum[:, j_cols], in_=e_sum[:, j_cols])
-            attention = soft_pool.tile([P, P], F32)
-            nc.gpsimd.tensor_tensor(out=attention[:], in0=enc_e_sum[:, j_cols], in1=e_sum[:, j_cols], op=ALU.mult)
             if jc == 0:
-                att_t_ps = psum_move.tile([P, PACK, P], F32, tag="move")
-                att_t_of[bt] = att_t_ps
-            nc.tensor.transpose(att_t_of[bt][:, jc, :], attention[:], ident_f32[:])
+                e_sum = row_pool.tile([P, H], F32)
+                e_sum_of[bt] = e_sum
+            nc.vector.tensor_reduce(
+                out=e_sum_of[bt][:, jc * P : (jc + 1) * P], in_=over_s(e_of[c][:]), axis=INNER_TWO, op=ALU.add
+            )
 
-        def cell_stage_0(bt):
+        def sum_enc_e(c):
+            bt, jc = divmod(c, N_JC)
+            if jc == 0:
+                enc_e_sum = row_pool.tile([P, H], F32)
+                enc_e_sum_of[bt] = enc_e_sum
+            nc.vector.tensor_reduce(
+                out=enc_e_sum_of[bt][:, jc * P : (jc + 1) * P], in_=over_s(enc_e_of[c][:]), axis=INNER_TWO, op=ALU.add
+            )
+
+        def one_over_e_sum(bt):
+            nc.scalar.activation(out=e_sum_of[bt][:], in_=e_sum_of[bt][:], func=FUNC.Ln)
+            nc.scalar.activation(out=e_sum_of[bt][:], in_=e_sum_of[bt][:], func=FUNC.Exp, scale=-1.0)
+
+        def attention(bt):
+            att = row_pool.tile([P, H], F32)
+            nc.gpsimd.tensor_tensor(out=att[:], in0=enc_e_sum_of[bt][:], in1=e_sum_of[bt][:], op=ALU.mult)
+            att_t_ps = psum_move.tile([P, PACK, P], F32, tag="move")
+            for t in range(PACK):
+                nc.tensor.transpose(att_t_ps[:, t, :], att[:, t * P : (t + 1) * P], ident_f32[:])
             att_grouped = row_pool.tile([P, P, PACK], BF16, align_bytes=64)
-            nc.scalar.copy(out=att_grouped[:], in_=att_t_of[bt][:].rearrange("p t b -> p b t"))
+            nc.scalar.copy(out=att_grouped[:], in_=att_t_ps[:].rearrange("p t b -> p b t"))
+            cell_of[bt, "att_grouped"] = att_grouped
+
+        def load_c(bt):
             c_raw = row_pool.tile([P, H], BF16)
             nc.sync.dma_start(out=c_raw[:], in_=c_prev[bt * P : (bt + 1) * P, :])
-            cell_of[bt, "att_grouped"] = att_grouped
             cell_of[bt, "c_raw"] = c_raw
 
         def quantise_attention(bt):
@@ -219,7 +230,7 @@ def tile_decoderlstm_pa_t_kernel(
             )
             cell_of[bt, "att_q"] = (att_words, att_scales)
 
-        def cell_stage_1(bt):
+        def gates(bt):
             att_words, att_scales = cell_of[bt, "att_q"]
             c_t_ps = psum_move.tile([P, N_JC, P], BF16, tag="move")
             for jc in range(N_JC):
@@ -258,6 +269,18 @@ def tile_decoderlstm_pa_t_kernel(
             cell_of[bt, "c_t_ps"] = c_t_ps
             cell_of[bt, "tanh_gate"] = tanh_gate
 
+        def kept_state(bt):
+            kept = cell_pool.tile([P, N_JC, P], F32)
+            nc.vector.scalar_tensor_tensor(
+                out=kept[:],
+                in0=cell_of[bt, "tanh_gate"][:, :, GATE_F, :],
+                scalar=1.0,
+                in1=cell_of[bt, "c_t_ps"][:],
+                op0=ALU.add,
+                op1=ALU.mult,
+            )
+            cell_of[bt, "kept"] = kept
+
         def store_half_of(twice, result_dram, bt):
             back_ps = psum_move.tile([P, H], F32, tag="move")
             for jc in range(N_JC):
@@ -266,29 +289,20 @@ def tile_decoderlstm_pa_t_kernel(
             nc.scalar.mul(out=result[:], in_=back_ps[:], mul=0.5)
             nc.sync.dma_start(out=result_dram[bt * P : (bt + 1) * P, :], in_=result[:])
 
-        def cell_stage_2(bt):
+        def new_state(bt):
             tanh_gate = cell_of[bt, "tanh_gate"]
-            kept = cell_pool.tile([P, N_JC, P], F32)
-            nc.vector.scalar_tensor_tensor(
-                out=kept[:],
-                in0=tanh_gate[:, :, GATE_F, :],
-                scalar=1.0,
-                in1=cell_of[bt, "c_t_ps"][:],
-                op0=ALU.add,
-                op1=ALU.mult,
-            )
             fresh = cell_pool.tile([P, N_JC, P], F32)
             nc.gpsimd.tensor_tensor(
                 out=fresh[:], in0=tanh_gate[:, :, GATE_I, :], in1=tanh_gate[:, :, GATE_G, :], op=ALU.mult
             )
             c_twice = cell_pool.tile([P, N_JC, P], F32)
-            nc.gpsimd.tensor_tensor(out=c_twice[:], in0=kept[:], in1=fresh[:], op=ALU.add)
+            nc.gpsimd.tensor_tensor(out=c_twice[:], in0=cell_of[bt, "kept"][:], in1=fresh[:], op=ALU.add)
             tanh_c = cell_pool.tile([P, N_JC, P], F32)
             nc.scalar.activation(out=tanh_c[:], in_=c_twice[:], func=FUNC.Tanh, scale=0.5)
             store_half_of(c_twice, out_1, bt)
             cell_of[bt, "tanh_c"] = tanh_c
 
-        def cell_stage_3(bt):
+        def new_output(bt):
             h_twice = cell_pool.tile([P, N_JC, P], F32)
             nc.gpsimd.tensor_tensor(
                 out=h_twice[:], in0=cell_of[bt, "tanh_gate"][:, :, GATE_O, :], in1=cell_of[bt, "tanh_c"][:], op=ALU.mult
@@ -309,44 +323,39 @@ def tile_decoderlstm_pa_t_kernel(
         later_grouped = []
 
         def share_of(step):
-            return range(min(step * PREP_PER_STEP, len(later)), min((step + 1) * PREP_PER_STEP, len(later)))
+            return range(min(max(step, 0) * PREP_PER_STEP, len(later)), min(max(step + 1, 0) * PREP_PER_STEP, len(later)))
+
+        def for_chunk(c, *stages):
+            if 0 <= c < N_CHUNKS:
+                for stage in stages:
+                    stage(c)
+
+        def for_tile(first_chunk, *stages):
+            bt, jc = divmod(first_chunk, N_JC)
+            if jc == 0 and 0 <= bt < N_BT:
+                for stage in stages:
+                    stage(bt)
 
         with tc.manual_schedule():
-            for item in first:
-                quantise(item, bring_k_to_partitions(item))
-            load_enc(0)
-            attn_lin_into_psum(0)
-            regroup_enc(0)
+            for block in first:
+                quantise(block, bring_k_to_partitions(block))
 
-            n_chunks = N_BT * N_JC
-            for step in range(n_chunks + CELL_LAG + 4):
-                if step + 1 < n_chunks:
-                    regroup_enc(step + 1)
-                bt, cell_stage = divmod(step - CELL_LAG, 4)
-                if step < n_chunks:
-                    scores(step)
-                if step >= 1:
-                    for n in share_of(step - 1):
-                        quantise(later[n], later_grouped[n])
-                if 0 <= bt < N_BT and cell_stage == 1:
-                    quantise_attention(bt)
-                if step < n_chunks:
-                    exp_of_shifted_scores(step)
-                if 0 <= step - 1 < n_chunks:
-                    sum_e_and_weigh_enc(step - 1)
-                if 0 <= step - 2 < n_chunks:
-                    attention_of(step - 2)
-                if 0 <= bt < N_BT:
-                    if cell_stage == 0:
-                        cell_stage_0(bt)
-                    if cell_stage == 1:
-                        cell_stage_1(bt)
-                    if cell_stage == 2:
-                        cell_stage_2(bt)
-                    if cell_stage == 3:
-                        cell_stage_3(bt)
-                if step % N_JC == 1 and step // N_JC + 1 < N_BT:
-                    load_enc(step // N_JC + 1)
-                    attn_lin_into_psum(step // N_JC + 1)
+            for step in range(-4, N_CHUNKS + 7):
+                for_tile(step + 4, load_enc, attn_lin_into_psum)
+                for_chunk(step + 2, regroup_enc)
+                for_chunk(step + 1, scores)
+                for n in share_of(step - 1):
+                    quantise(later[n], later_grouped[n])
+                for_tile(step - 7, quantise_attention)
+                for_chunk(step + 1, max_over_s)
+                for_chunk(step, subtract_max, exponential)
+                for_chunk(step - 1, weigh_enc, sum_e)
+                for_chunk(step - 2, sum_enc_e)
+                for_tile(step - 5, one_over_e_sum, load_c)
+                for_tile(step - 6, attention)
+                for_tile(step - 7, gates)
+                for_tile(step - 8, kept_state)
+                for_tile(step - 9, new_state)
+                for_tile(step - 10, new_output)
                 for n in share_of(step):
                     later_grouped.append(bring_k_to_partitions(later[n]))

@@ -26,7 +26,6 @@ N_GC = N_GATES * N_JC
 S_RUN = 4
 S_OUT = S // S_RUN
 GATE_SCALE = (0.5, 0.5, 1.0, 0.5)
-PREP_PER_STEP = 6
 
 FLOPS = 2 * B * H * H + 2 * B * (3 * H) * (N_GATES * H)
 
@@ -37,11 +36,11 @@ def tile_decoderlstm_pa_t_kernel(
     nc = tc.nc
     with ExitStack() as ctx:
         keep = ctx.enter_context(tc.tile_pool(name="keep", bufs=1))
-        raw_pool = ctx.enter_context(tc.tile_pool(name="raw", bufs=4))
-        grouped_pool = ctx.enter_context(tc.tile_pool(name="grouped", bufs=PREP_PER_STEP + 2))
+        raw_pool = ctx.enter_context(tc.tile_pool(name="raw", bufs=2))
+        grouped_pool = ctx.enter_context(tc.tile_pool(name="grouped", bufs=3))
         enc_pool = ctx.enter_context(tc.tile_pool(name="enc", bufs=2))
         soft_pool = ctx.enter_context(tc.tile_pool(name="soft", bufs=4))
-        prod_pool = ctx.enter_context(tc.tile_pool(name="prod", bufs=3))
+        prod_pool = ctx.enter_context(tc.tile_pool(name="prod", bufs=2))
         row_pool = ctx.enter_context(tc.tile_pool(name="row", bufs=2))
         cell_pool = ctx.enter_context(tc.tile_pool(name="cell", bufs=1))
         out_pool = ctx.enter_context(tc.tile_pool(name="out", bufs=2))
@@ -86,23 +85,24 @@ def tile_decoderlstm_pa_t_kernel(
         w_att_q = operand_tiles(N_GC, "w_att")
         w_h_q = operand_tiles(N_GC, "w_h")
 
-        def bring_k_to_partitions(block):
-            matrix, k_cols, operand, pair = block
-            rows = matrix[2 * P * pair : 2 * P * (pair + 1), k_cols]
-            raw = raw_pool.tile([P, 2, K_PASS], BF16)
+        def bring_k_to_partitions(group):
+            matrix, k_cols, operand, first_chunk, n_chunks = group
+            rows = matrix[first_chunk * P : (first_chunk + n_chunks) * P, k_cols]
+            raw = raw_pool.tile([P, n_chunks, K_PASS], BF16)
             nc.sync.dma_start(out=raw[:], in_=rows.rearrange("(a r) k -> r a k", r=P))
-            k_first = psum_move.tile([P, 2, PACK, P], BF16, tag="move")
-            for a in range(2):
-                for t in range(PACK):
-                    nc.tensor.transpose(k_first[:, a, t, :], raw[:, a, t * P : (t + 1) * P], ident_bf[:])
-            grouped = grouped_pool.tile([P, 2, P, PACK], BF16, align_bytes=64)
-            nc.scalar.copy(out=grouped[:], in_=k_first[:].rearrange("p a t r -> p a r t"))
+            grouped = grouped_pool.tile([P, n_chunks, P, PACK], BF16, align_bytes=64)
+            for a0 in range(0, n_chunks, 2):
+                k_first = psum_move.tile([P, 2, PACK, P], BF16, tag="move")
+                for a in range(2):
+                    for t in range(PACK):
+                        nc.tensor.transpose(k_first[:, a, t, :], raw[:, a0 + a, t * P : (t + 1) * P], ident_bf[:])
+                nc.scalar.copy(out=grouped[:, a0 : a0 + 2, :, :], in_=k_first[:].rearrange("p a t r -> p a r t"))
             return grouped
 
-        def quantise(block, grouped):
-            matrix, k_cols, operand, pair = block
+        def quantise(group, grouped):
+            matrix, k_cols, operand, first_chunk, n_chunks = group
             words, scales = operand
-            chunks = slice(2 * pair, 2 * pair + 2)
+            chunks = slice(first_chunk, first_chunk + n_chunks)
             nc.vector.quantize_mx(
                 out=words[:, chunks, :].rearrange("p a r -> p (a r)").bitcast(FP8X4),
                 scales=scales[:, chunks, :].rearrange("p a r -> p (a r)"),
@@ -201,18 +201,30 @@ def tile_decoderlstm_pa_t_kernel(
                 out=enc_e_sum_of[bt][:, jc * P : (jc + 1) * P], in_=over_s(enc_e_of[c][:]), axis=INNER_TWO, op=ALU.add
             )
 
+        def transposed_into_psum(row_tile):
+            t_ps = psum_move.tile([P, PACK, P], F32, tag="move")
+            for t in range(PACK):
+                nc.tensor.transpose(t_ps[:, t, :], row_tile[:, t * P : (t + 1) * P], ident_f32[:])
+            return t_ps
+
         def one_over_e_sum(bt):
-            nc.scalar.activation(out=e_sum_of[bt][:], in_=e_sum_of[bt][:], func=FUNC.Ln)
-            nc.scalar.activation(out=e_sum_of[bt][:], in_=e_sum_of[bt][:], func=FUNC.Exp, scale=-1.0)
+            e_sum_t_ps = transposed_into_psum(e_sum_of[bt])
+            inv_t = row_pool.tile([P, PACK, P], F32)
+            nc.scalar.activation(out=inv_t[:], in_=e_sum_t_ps[:], func=FUNC.Ln)
+            nc.scalar.activation(out=inv_t[:], in_=inv_t[:], func=FUNC.Exp, scale=-1.0)
+            cell_of[bt, "inv_t"] = inv_t
+
+        def transpose_enc_e_sum(bt):
+            cell_of[bt, "enc_e_sum_t_ps"] = transposed_into_psum(enc_e_sum_of[bt])
 
         def attention(bt):
-            att = row_pool.tile([P, H], F32)
-            nc.gpsimd.tensor_tensor(out=att[:], in0=enc_e_sum_of[bt][:], in1=e_sum_of[bt][:], op=ALU.mult)
-            att_t_ps = psum_move.tile([P, PACK, P], F32, tag="move")
-            for t in range(PACK):
-                nc.tensor.transpose(att_t_ps[:, t, :], att[:, t * P : (t + 1) * P], ident_f32[:])
             att_grouped = row_pool.tile([P, P, PACK], BF16, align_bytes=64)
-            nc.scalar.copy(out=att_grouped[:], in_=att_t_ps[:].rearrange("p t b -> p b t"))
+            nc.vector.tensor_tensor(
+                out=att_grouped[:],
+                in0=cell_of[bt, "enc_e_sum_t_ps"][:].rearrange("p t b -> p b t"),
+                in1=cell_of[bt, "inv_t"][:].rearrange("p t b -> p b t"),
+                op=ALU.mult,
+            )
             cell_of[bt, "att_grouped"] = att_grouped
 
         def load_c(bt):
@@ -264,66 +276,81 @@ def tile_decoderlstm_pa_t_kernel(
                         bias=gate_bias[:, gc : gc + 1],
                         scale=GATE_SCALE[gate],
                     )
-            for gate in (GATE_I, GATE_O):
-                nc.scalar.add(out=tanh_gate[:, :, gate, :], in_=tanh_gate[:, :, gate, :], add=1.0)
+            nc.scalar.add(out=tanh_gate[:, :, GATE_O, :], in_=tanh_gate[:, :, GATE_O, :], add=1.0)
+            tanh_g_ps = psum_move.tile([P, N_JC, P], F32, tag="move")
+            nc.tensor.matmul(out=tanh_g_ps[:], lhsT=ident_f32[:], rhs=tanh_gate[:, :, GATE_G, :], start=True, stop=True)
             cell_of[bt, "c_t_ps"] = c_t_ps
+            cell_of[bt, "tanh_g_ps"] = tanh_g_ps
             cell_of[bt, "tanh_gate"] = tanh_gate
 
-        def kept_state(bt):
+        def kept_and_fresh(bt):
+            tanh_gate = cell_of[bt, "tanh_gate"]
             kept = cell_pool.tile([P, N_JC, P], F32)
             nc.vector.scalar_tensor_tensor(
                 out=kept[:],
-                in0=cell_of[bt, "tanh_gate"][:, :, GATE_F, :],
+                in0=tanh_gate[:, :, GATE_F, :],
                 scalar=1.0,
                 in1=cell_of[bt, "c_t_ps"][:],
                 op0=ALU.add,
                 op1=ALU.mult,
             )
+            fresh = cell_pool.tile([P, N_JC, P], F32)
+            nc.vector.scalar_tensor_tensor(
+                out=fresh[:],
+                in0=tanh_gate[:, :, GATE_I, :],
+                scalar=1.0,
+                in1=cell_of[bt, "tanh_g_ps"][:],
+                op0=ALU.add,
+                op1=ALU.mult,
+            )
             cell_of[bt, "kept"] = kept
-
-        def store_half_of(twice, result_dram, bt):
-            back_ps = psum_move.tile([P, H], F32, tag="move")
-            for jc in range(N_JC):
-                nc.tensor.transpose(back_ps[:, jc * P : (jc + 1) * P], twice[:, jc, :], ident_f32[:])
-            result = out_pool.tile([P, H], F32)
-            nc.scalar.mul(out=result[:], in_=back_ps[:], mul=0.5)
-            nc.sync.dma_start(out=result_dram[bt * P : (bt + 1) * P, :], in_=result[:])
+            cell_of[bt, "fresh"] = fresh
 
         def new_state(bt):
+            b_rows = slice(bt * P, (bt + 1) * P)
             tanh_gate = cell_of[bt, "tanh_gate"]
-            fresh = cell_pool.tile([P, N_JC, P], F32)
-            nc.gpsimd.tensor_tensor(
-                out=fresh[:], in0=tanh_gate[:, :, GATE_I, :], in1=tanh_gate[:, :, GATE_G, :], op=ALU.mult
-            )
-            c_twice = cell_pool.tile([P, N_JC, P], F32)
-            nc.gpsimd.tensor_tensor(out=c_twice[:], in0=cell_of[bt, "kept"][:], in1=fresh[:], op=ALU.add)
-            tanh_c = cell_pool.tile([P, N_JC, P], F32)
-            nc.scalar.activation(out=tanh_c[:], in_=c_twice[:], func=FUNC.Tanh, scale=0.5)
-            store_half_of(c_twice, out_1, bt)
+            kept = cell_of[bt, "kept"]
+            fresh = cell_of[bt, "fresh"]
+            c_twice_ps = psum_move.tile([P, H], F32, tag="move")
+            for jc in range(N_JC):
+                j_cols = slice(jc * P, (jc + 1) * P)
+                nc.tensor.matmul(out=c_twice_ps[:, j_cols], lhsT=kept[:, jc, :], rhs=ident_f32[:], start=True, stop=False)
+                nc.tensor.matmul(out=c_twice_ps[:, j_cols], lhsT=fresh[:, jc, :], rhs=ident_f32[:], start=False, stop=True)
+            c_new = out_pool.tile([P, H], F32)
+            nc.scalar.mul(out=c_new[:], in_=c_twice_ps[:], mul=0.5)
+            nc.sync.dma_start(out=out_1[b_rows, :], in_=c_new[:])
+            tanh_c = cell_pool.tile([P, H], F32)
+            nc.scalar.activation(out=tanh_c[:], in_=c_twice_ps[:], func=FUNC.Tanh, scale=0.5)
+            o_twice_ps = psum_move.tile([P, H], F32, tag="move")
+            for jc in range(N_JC):
+                nc.tensor.transpose(o_twice_ps[:, jc * P : (jc + 1) * P], tanh_gate[:, jc, GATE_O, :], ident_f32[:])
             cell_of[bt, "tanh_c"] = tanh_c
+            cell_of[bt, "o_twice_ps"] = o_twice_ps
 
         def new_output(bt):
-            h_twice = cell_pool.tile([P, N_JC, P], F32)
-            nc.gpsimd.tensor_tensor(
-                out=h_twice[:], in0=cell_of[bt, "tanh_gate"][:, :, GATE_O, :], in1=cell_of[bt, "tanh_c"][:], op=ALU.mult
+            h_new = out_pool.tile([P, H], F32)
+            nc.vector.scalar_tensor_tensor(
+                out=h_new[:],
+                in0=cell_of[bt, "o_twice_ps"][:],
+                scalar=0.5,
+                in1=cell_of[bt, "tanh_c"][:],
+                op0=ALU.mult,
+                op1=ALU.mult,
             )
-            store_half_of(h_twice, out_0, bt)
+            nc.sync.dma_start(out=out_0[bt * P : (bt + 1) * P, :], in_=h_new[:])
 
         first_half = slice(0, H)
         second_half = slice(H, 2 * H)
-        first = [(x, first_half, x_q, 0)] + [(attn_W, first_half, attn_w_q, pair) for pair in range(N_JC // 2)]
-        later = [(x, first_half, x_q, pair) for pair in range(1, N_BT // 2)]
-        later += [(h_prev, first_half, h_q, pair) for pair in range(N_BT // 2)]
-        for pair in range(N_GC // 2):
+        half_batch = N_BT // 2
+        first = [(x, first_half, x_q, 0, half_batch), (attn_W, first_half, attn_w_q, 0, N_JC)]
+        later = [(x, first_half, x_q, half_batch, half_batch), (h_prev, first_half, h_q, 0, N_BT)]
+        for first_chunk in range(0, N_GC, 8):
             later += [
-                (W_ih0, first_half, w_x_q, pair),
-                (W_hh0, first_half, w_h_q, pair),
-                (W_ih0, second_half, w_att_q, pair),
+                (W_ih0, first_half, w_x_q, first_chunk, 8),
+                (W_hh0, first_half, w_h_q, first_chunk, 8),
+                (W_ih0, second_half, w_att_q, first_chunk, 8),
             ]
         later_grouped = []
-
-        def share_of(step):
-            return range(min(max(step, 0) * PREP_PER_STEP, len(later)), min(max(step + 1, 0) * PREP_PER_STEP, len(later)))
 
         def for_chunk(c, *stages):
             if 0 <= c < N_CHUNKS:
@@ -337,25 +364,24 @@ def tile_decoderlstm_pa_t_kernel(
                     stage(bt)
 
         with tc.manual_schedule():
-            for block in first:
-                quantise(block, bring_k_to_partitions(block))
+            for group in first:
+                quantise(group, bring_k_to_partitions(group))
 
-            for step in range(-4, N_CHUNKS + 7):
+            for step in range(-4, N_CHUNKS + 8):
                 for_tile(step + 4, load_enc, attn_lin_into_psum)
                 for_chunk(step + 2, regroup_enc)
-                for_chunk(step + 1, scores)
-                for n in share_of(step - 1):
-                    quantise(later[n], later_grouped[n])
-                for_tile(step - 7, quantise_attention)
-                for_chunk(step + 1, max_over_s)
+                for_chunk(step + 1, scores, max_over_s)
+                for_tile(step - 7, attention, quantise_attention)
+                if 0 <= step - 1 < len(later):
+                    quantise(later[step - 1], later_grouped[step - 1])
                 for_chunk(step, subtract_max, exponential)
                 for_chunk(step - 1, weigh_enc, sum_e)
                 for_chunk(step - 2, sum_enc_e)
                 for_tile(step - 5, one_over_e_sum, load_c)
-                for_tile(step - 6, attention)
-                for_tile(step - 7, gates)
-                for_tile(step - 8, kept_state)
-                for_tile(step - 9, new_state)
-                for_tile(step - 10, new_output)
-                for n in share_of(step):
-                    later_grouped.append(bring_k_to_partitions(later[n]))
+                for_tile(step - 6, transpose_enc_e_sum)
+                for_tile(step - 8, gates)
+                for_tile(step - 9, kept_and_fresh)
+                for_tile(step - 10, new_state)
+                for_tile(step - 11, new_output)
+                if 0 <= step < len(later):
+                    later_grouped.append(bring_k_to_partitions(later[step]))

from contextlib import ExitStack

import concourse.mybir as mybir
from concourse.masks import make_identity

BF16 = mybir.dt.bfloat16
F32 = mybir.dt.float32
U32 = mybir.dt.uint32
U8 = mybir.dt.uint8
I32 = mybir.dt.int32
FP8X4 = mybir.dt.float8_e4m3fn_x4
ALU = mybir.AluOpType
FUNC = mybir.ActivationFunctionType
INNER_TWO = mybir.AxisListType.XY

P = 128
PACK = 4
K_PASS = P * PACK
B, H, S = 1024, 512, 16
N_BT = B // P
N_JC = H // P
N_CHUNKS = N_BT * N_JC
N_GATES = 4
GATE_I, GATE_F, GATE_G, GATE_O = 0, 1, 2, 3
N_GC = N_GATES * N_JC
S_RUN = 4
S_OUT = S // S_RUN
GATE_SCALE = (0.5, 0.5, 1.0, 0.5)

FLOPS = 2 * B * H * H + 2 * B * (3 * H) * (N_GATES * H)


def tile_decoderlstm_pa_t_kernel(
    tc, x, enc_seq, attn_W, attn_b, h_prev, c_prev, W_ih0, W_hh0, b_ih0, b_hh0, out_0, out_1
):
    nc = tc.nc
    with ExitStack() as ctx:
        keep = ctx.enter_context(tc.tile_pool(name="keep", bufs=1))
        raw_pool = ctx.enter_context(tc.tile_pool(name="raw", bufs=2))
        grouped_pool = ctx.enter_context(tc.tile_pool(name="grouped", bufs=3))
        enc_pool = ctx.enter_context(tc.tile_pool(name="enc", bufs=2))
        soft_pool = ctx.enter_context(tc.tile_pool(name="soft", bufs=4))
        prod_pool = ctx.enter_context(tc.tile_pool(name="prod", bufs=2))
        row_pool = ctx.enter_context(tc.tile_pool(name="row", bufs=2))
        cell_pool = ctx.enter_context(tc.tile_pool(name="cell", bufs=1))
        out_pool = ctx.enter_context(tc.tile_pool(name="out", bufs=2))
        psum_lin = ctx.enter_context(tc.psum_pool(name="psum_lin", bufs=2))
        psum_gates = ctx.enter_context(tc.psum_pool(name="psum_gates", bufs=2))
        psum_move = ctx.enter_context(tc.psum_pool(name="psum_move", bufs=4))

        ident_bf = keep.tile([P, P], BF16)
        make_identity(nc, ident_bf[:])
        ident_f32 = keep.tile([P, P], F32)
        make_identity(nc, ident_f32[:])

        bias_rows = keep.tile([P, P], BF16)
        nc.vector.memset(bias_rows[:].bitcast(I32), 0)
        nc.sync.dma_start(out=bias_rows[0:N_GC, :], in_=b_ih0.rearrange("(r c) -> r c", c=P))
        nc.sync.dma_start(out=bias_rows[N_GC : 2 * N_GC, :], in_=b_hh0.rearrange("(r c) -> r c", c=P))
        nc.sync.dma_start(
            out=bias_rows[2 * N_GC : 2 * N_GC + N_JC, :], in_=attn_b.rearrange("(r c) -> r c", c=P)
        )
        bias_ps = psum_move.tile([P, P], BF16, tag="move")
        nc.tensor.transpose(bias_ps[:], bias_rows[:], ident_bf[:])
        bias_cols = keep.tile([P, P], F32)
        nc.scalar.copy(out=bias_cols[:], in_=bias_ps[:])
        attn_bias = bias_cols[:, 2 * N_GC : 2 * N_GC + N_JC]
        gate_bias = keep.tile([P, N_GC], F32)
        nc.vector.tensor_tensor(
            out=gate_bias[:], in0=bias_cols[:, 0:N_GC], in1=bias_cols[:, N_GC : 2 * N_GC], op=ALU.add
        )
        for gate in range(N_GATES):
            cols = slice(gate * N_JC, (gate + 1) * N_JC)
            nc.vector.tensor_scalar_mul(out=gate_bias[:, cols], in0=gate_bias[:, cols], scalar1=GATE_SCALE[gate])

        def operand_tiles(n_chunks, label):
            words = keep.tile([P, n_chunks, P], U32, name=label + "_words", align_bytes=64)
            scales = keep.tile([P, n_chunks, P], U8, name=label + "_scales", align_bytes=64)
            return words, scales

        x_q = operand_tiles(N_BT, "x")
        h_q = operand_tiles(N_BT, "h")
        attn_w_q = operand_tiles(N_JC, "attn_w")
        w_x_q = operand_tiles(N_GC, "w_x")
        w_att_q = operand_tiles(N_GC, "w_att")
        w_h_q = operand_tiles(N_GC, "w_h")

        def bring_k_to_partitions(group):
            matrix, k_cols, operand, first_chunk, n_chunks = group
            rows = matrix[first_chunk * P : (first_chunk + n_chunks) * P, k_cols]
            raw = raw_pool.tile([P, n_chunks, K_PASS], BF16)
            nc.sync.dma_start(out=raw[:], in_=rows.rearrange("(a r) k -> r a k", r=P))
            grouped = grouped_pool.tile([P, n_chunks, P, PACK], BF16, align_bytes=64)
            for a0 in range(0, n_chunks, 2):
                k_first = psum_move.tile([P, 2, PACK, P], BF16, tag="move")
                for a in range(2):
                    for t in range(PACK):
                        nc.tensor.transpose(k_first[:, a, t, :], raw[:, a0 + a, t * P : (t + 1) * P], ident_bf[:])
                nc.scalar.copy(out=grouped[:, a0 : a0 + 2, :, :], in_=k_first[:].rearrange("p a t r -> p a r t"))
            return grouped

        def quantise(group, grouped):
            matrix, k_cols, operand, first_chunk, n_chunks = group
            words, scales = operand
            chunks = slice(first_chunk, first_chunk + n_chunks)
            nc.vector.quantize_mx(
                out=words[:, chunks, :].rearrange("p a r -> p (a r)").bitcast(FP8X4),
                scales=scales[:, chunks, :].rearrange("p a r -> p (a r)"),
                in_=grouped[:].rearrange("p a r t -> p (a r t)"),
            )

        enc_of, enc_r_of, lin_of, e_of, top_of, enc_e_of = {}, {}, {}, {}, {}, {}
        e_sum_of, enc_e_sum_of, cell_of = {}, {}, {}

        def load_enc(bt):
            enc_sb = enc_pool.tile([P, S, H], BF16)
            nc.sync.dma_start(
                out=enc_sb[:], in_=enc_seq[:, bt * P : (bt + 1) * P, :].rearrange("s b j -> b s j")
            )
            enc_of[bt] = enc_sb

        def attn_lin_into_psum(bt):
            lin_t_ps = psum_move.tile([P, N_JC, P], F32, tag="move")
            for jc in range(N_JC):
                nc.tensor.matmul_mx(
                    out=lin_t_ps[:, jc, :],
                    lhsT=attn_w_q[0][:, jc, :].bitcast(FP8X4),
                    lhsT_scale=attn_w_q[1][:, jc, :],
                    rhs=x_q[0][:, bt, :].bitcast(FP8X4),
                    rhs_scale=x_q[1][:, bt, :],
                    start=True,
                    stop=True,
                )
            lin_t = row_pool.tile([P, N_JC, P], F32)
            for jc in range(N_JC):
                nc.scalar.activation(
                    out=lin_t[:, jc, :], in_=lin_t_ps[:, jc, :], func=FUNC.Identity, bias=attn_bias[:, jc : jc + 1]
                )
            lin_ps = psum_lin.tile([P, H], F32)
            for jc in range(N_JC):
                nc.tensor.transpose(lin_ps[:, jc * P : (jc + 1) * P], lin_t[:, jc, :], ident_f32[:])
            lin_of[bt] = lin_ps

        soft_shape = [P, S_OUT, P, S_RUN]

        def over_s(tile_ap):
            return tile_ap.rearrange("p o j r -> p j o r")

        def for_all_s(row_ap):
            return row_ap.unsqueeze(1).unsqueeze(3).to_broadcast(soft_shape)

        def regroup_enc(c):
            bt, jc = divmod(c, N_JC)
            enc_r = soft_pool.tile(soft_shape, BF16)
            nc.scalar.copy(
                out=enc_r[:],
                in_=enc_of[bt][:, :, jc * P : (jc + 1) * P].rearrange("p (o r) j -> p o j r", r=S_RUN),
            )
            enc_r_of[c] = enc_r

        def scores(c):
            bt, jc = divmod(c, N_JC)
            e = soft_pool.tile(soft_shape, F32)
            nc.vector.tensor_tensor(
                out=e[:], in0=for_all_s(lin_of[bt][:, jc * P : (jc + 1) * P]), in1=enc_r_of[c][:], op=ALU.mult
            )
            e_of[c] = e

        def max_over_s(c):
            top = soft_pool.tile([P, P], F32)
            nc.vector.tensor_reduce(out=top[:], in_=over_s(e_of[c][:]), axis=INNER_TWO, op=ALU.max)
            top_of[c] = top

        def subtract_max(c):
            nc.gpsimd.tensor_tensor(out=e_of[c][:], in0=e_of[c][:], in1=for_all_s(top_of[c][:]), op=ALU.subtract)

        def exponential(c):
            e_flat = e_of[c][:].rearrange("p o j r -> p (o j r)")
            nc.scalar.activation(out=e_flat, in_=e_flat, func=FUNC.Exp)

        def weigh_enc(c):
            enc_e = prod_pool.tile(soft_shape, F32)
            nc.gpsimd.tensor_tensor(out=enc_e[:], in0=enc_r_of[c][:], in1=e_of[c][:], op=ALU.mult)
            enc_e_of[c] = enc_e

        def sum_e(c):
            bt, jc = divmod(c, N_JC)
            if jc == 0:
                e_sum = row_pool.tile([P, H], F32)
                e_sum_of[bt] = e_sum
            nc.vector.tensor_reduce(
                out=e_sum_of[bt][:, jc * P : (jc + 1) * P], in_=over_s(e_of[c][:]), axis=INNER_TWO, op=ALU.add
            )

        def sum_enc_e(c):
            bt, jc = divmod(c, N_JC)
            if jc == 0:
                enc_e_sum = row_pool.tile([P, H], F32)
                enc_e_sum_of[bt] = enc_e_sum
            nc.vector.tensor_reduce(
                out=enc_e_sum_of[bt][:, jc * P : (jc + 1) * P], in_=over_s(enc_e_of[c][:]), axis=INNER_TWO, op=ALU.add
            )

        def transposed_into_psum(row_tile):
            t_ps = psum_move.tile([P, PACK, P], F32, tag="move")
            for t in range(PACK):
                nc.tensor.transpose(t_ps[:, t, :], row_tile[:, t * P : (t + 1) * P], ident_f32[:])
            return t_ps

        def one_over_e_sum(bt):
            e_sum_t_ps = transposed_into_psum(e_sum_of[bt])
            inv_t = row_pool.tile([P, PACK, P], F32)
            nc.scalar.activation(out=inv_t[:], in_=e_sum_t_ps[:], func=FUNC.Ln)
            nc.scalar.activation(out=inv_t[:], in_=inv_t[:], func=FUNC.Exp, scale=-1.0)
            cell_of[bt, "inv_t"] = inv_t

        def transpose_enc_e_sum(bt):
            cell_of[bt, "enc_e_sum_t_ps"] = transposed_into_psum(enc_e_sum_of[bt])

        def attention(bt):
            att_grouped = row_pool.tile([P, P, PACK], BF16, align_bytes=64)
            nc.vector.tensor_tensor(
                out=att_grouped[:],
                in0=cell_of[bt, "enc_e_sum_t_ps"][:].rearrange("p t b -> p b t"),
                in1=cell_of[bt, "inv_t"][:].rearrange("p t b -> p b t"),
                op=ALU.mult,
            )
            cell_of[bt, "att_grouped"] = att_grouped

        def load_c(bt):
            c_raw = row_pool.tile([P, H], BF16)
            nc.sync.dma_start(out=c_raw[:], in_=c_prev[bt * P : (bt + 1) * P, :])
            cell_of[bt, "c_raw"] = c_raw

        def quantise_attention(bt):
            att_words = row_pool.tile([P, P], U32, align_bytes=64)
            att_scales = row_pool.tile([P, P], U8, align_bytes=64)
            nc.vector.quantize_mx(
                out=att_words[:].bitcast(FP8X4),
                scales=att_scales[:],
                in_=cell_of[bt, "att_grouped"][:].rearrange("p b t -> p (b t)"),
            )
            cell_of[bt, "att_q"] = (att_words, att_scales)

        def gates(bt):
            att_words, att_scales = cell_of[bt, "att_q"]
            c_t_ps = psum_move.tile([P, N_JC, P], BF16, tag="move")
            for jc in range(N_JC):
                nc.tensor.transpose(c_t_ps[:, jc, :], cell_of[bt, "c_raw"][:, jc * P : (jc + 1) * P], ident_bf[:])
            products = (
                (w_x_q, x_q[0][:, bt, :], x_q[1][:, bt, :]),
                (w_h_q, h_q[0][:, bt, :], h_q[1][:, bt, :]),
                (w_att_q, att_words[:], att_scales[:]),
            )
            tanh_gate = cell_pool.tile([P, N_JC, N_GATES, P], F32)
            for jc in range(N_JC):
                gates_ps = psum_gates.tile([P, N_GATES, P], F32)
                for gate in range(N_GATES):
                    gc = gate * N_JC + jc
                    for i, (weights, v_words, v_scales) in enumerate(products):
                        nc.tensor.matmul_mx(
                            out=gates_ps[:, gate, :],
                            lhsT=weights[0][:, gc, :].bitcast(FP8X4),
                            lhsT_scale=weights[1][:, gc, :],
                            rhs=v_words.bitcast(FP8X4),
                            rhs_scale=v_scales,
                            start=(i == 0),
                            stop=(i == len(products) - 1),
                        )
                for gate in range(N_GATES):
                    gc = gate * N_JC + jc
                    nc.scalar.activation(
                        out=tanh_gate[:, jc, gate, :],
                        in_=gates_ps[:, gate, :],
                        func=FUNC.Tanh,
                        bias=gate_bias[:, gc : gc + 1],
                        scale=GATE_SCALE[gate],
                    )
            nc.scalar.add(out=tanh_gate[:, :, GATE_O, :], in_=tanh_gate[:, :, GATE_O, :], add=1.0)
            tanh_g_ps = psum_move.tile([P, N_JC, P], F32, tag="move")
            nc.tensor.matmul(out=tanh_g_ps[:], lhsT=ident_f32[:], rhs=tanh_gate[:, :, GATE_G, :], start=True, stop=True)
            cell_of[bt, "c_t_ps"] = c_t_ps
            cell_of[bt, "tanh_g_ps"] = tanh_g_ps
            cell_of[bt, "tanh_gate"] = tanh_gate

        def kept_and_fresh(bt):
            tanh_gate = cell_of[bt, "tanh_gate"]
            kept = cell_pool.tile([P, N_JC, P], F32)
            nc.vector.scalar_tensor_tensor(
                out=kept[:],
                in0=tanh_gate[:, :, GATE_F, :],
                scalar=1.0,
                in1=cell_of[bt, "c_t_ps"][:],
                op0=ALU.add,
                op1=ALU.mult,
            )
            fresh = cell_pool.tile([P, N_JC, P], F32)
            nc.vector.scalar_tensor_tensor(
                out=fresh[:],
                in0=tanh_gate[:, :, GATE_I, :],
                scalar=1.0,
                in1=cell_of[bt, "tanh_g_ps"][:],
                op0=ALU.add,
                op1=ALU.mult,
            )
            cell_of[bt, "kept"] = kept
            cell_of[bt, "fresh"] = fresh

        def new_state(bt):
            b_rows = slice(bt * P, (bt + 1) * P)
            tanh_gate = cell_of[bt, "tanh_gate"]
            kept = cell_of[bt, "kept"]
            fresh = cell_of[bt, "fresh"]
            c_twice_ps = psum_move.tile([P, H], F32, tag="move")
            for jc in range(N_JC):
                j_cols = slice(jc * P, (jc + 1) * P)
                nc.tensor.matmul(out=c_twice_ps[:, j_cols], lhsT=kept[:, jc, :], rhs=ident_f32[:], start=True, stop=False)
                nc.tensor.matmul(out=c_twice_ps[:, j_cols], lhsT=fresh[:, jc, :], rhs=ident_f32[:], start=False, stop=True)
            c_new = out_pool.tile([P, H], F32)
            nc.scalar.mul(out=c_new[:], in_=c_twice_ps[:], mul=0.5)
            nc.sync.dma_start(out=out_1[b_rows, :], in_=c_new[:])
            tanh_c = cell_pool.tile([P, H], F32)
            nc.scalar.activation(out=tanh_c[:], in_=c_twice_ps[:], func=FUNC.Tanh, scale=0.5)
            o_twice_ps = psum_move.tile([P, H], F32, tag="move")
            for jc in range(N_JC):
                nc.tensor.transpose(o_twice_ps[:, jc * P : (jc + 1) * P], tanh_gate[:, jc, GATE_O, :], ident_f32[:])
            cell_of[bt, "tanh_c"] = tanh_c
            cell_of[bt, "o_twice_ps"] = o_twice_ps

        def new_output(bt):
            h_new = out_pool.tile([P, H], F32)
            nc.vector.scalar_tensor_tensor(
                out=h_new[:],
                in0=cell_of[bt, "o_twice_ps"][:],
                scalar=0.5,
                in1=cell_of[bt, "tanh_c"][:],
                op0=ALU.mult,
                op1=ALU.mult,
            )
            nc.sync.dma_start(out=out_0[bt * P : (bt + 1) * P, :], in_=h_new[:])

        first_half = slice(0, H)
        second_half = slice(H, 2 * H)
        half_batch = N_BT // 2
        first = [(x, first_half, x_q, 0, half_batch), (attn_W, first_half, attn_w_q, 0, N_JC)]
        later = [(x, first_half, x_q, half_batch, half_batch), (h_prev, first_half, h_q, 0, N_BT)]
        for first_chunk in range(0, N_GC, 8):
            later += [
                (W_ih0, first_half, w_x_q, first_chunk, 8),
                (W_hh0, first_half, w_h_q, first_chunk, 8),
                (W_ih0, second_half, w_att_q, first_chunk, 8),
            ]
        later_grouped = []

        def for_chunk(c, *stages):
            if 0 <= c < N_CHUNKS:
                for stage in stages:
                    stage(c)

        def for_tile(first_chunk, *stages):
            bt, jc = divmod(first_chunk, N_JC)
            if jc == 0 and 0 <= bt < N_BT:
                for stage in stages:
                    stage(bt)

        with tc.manual_schedule():
            for group in first:
                quantise(group, bring_k_to_partitions(group))

            for step in range(-4, N_CHUNKS + 8):
                for_tile(step + 4, load_enc, attn_lin_into_psum)
                for_chunk(step + 2, regroup_enc)
                for_chunk(step + 1, scores, max_over_s)
                for_tile(step - 7, attention, quantise_attention)
                if 0 <= step - 1 < len(later):
                    quantise(later[step - 1], later_grouped[step - 1])
                for_chunk(step, subtract_max, exponential)
                for_chunk(step - 1, weigh_enc, sum_e)
                for_chunk(step - 2, sum_enc_e)
                for_tile(step - 5, one_over_e_sum, load_c)
                for_tile(step - 6, transpose_enc_e_sum)
                for_tile(step - 8, gates)
                for_tile(step - 9, kept_and_fresh)
                for_tile(step - 10, new_state)
                for_tile(step - 11, new_output)
                if 0 <= step < len(later):
                    later_grouped.append(bring_k_to_partitions(later[step]))
